import numpy as np
import ml_dtypes


def mxq(x, axis, fmt="e4m3"):
    dtype, down = {"e4m3": (ml_dtypes.float8_e4m3fn, 7), "e5m2": (ml_dtypes.float8_e5m2, 14)}[fmt]
    v = np.moveaxis(np.asarray(x, np.float32).astype(ml_dtypes.bfloat16).astype(np.float64), axis, -1)
    blocks = v.reshape(v.shape[:-1] + (-1, 32))
    amax = np.abs(blocks).max(-1, keepdims=True)
    byte = np.maximum(np.where(amax > 0, np.frexp(amax)[1] - 1 + 127, 0) - down, 1)
    scale = np.exp2(byte - 127.0)
    codes = (blocks / scale).astype(np.float32).astype(dtype).astype(np.float64)
    return np.moveaxis((codes * scale).reshape(v.shape), -1, axis)


WIDE = False


def mx_kscale(k):
    if not WIDE:
        return np.ones(k)
    levels = np.array([10, -10, 5, -5, 0])
    if k % 512:
        return np.exp2(np.random.permutation(np.resize(levels, k // 32))).repeat(32)
    a = np.empty((k // 512, 16))
    for p in range(k // 512):
        a[p, :8] = np.random.permutation(np.resize(levels, 8))
        for g in range(8):
            far = levels[np.abs(levels - a[p, g]) >= 10]
            a[p, g + 8] = far[np.random.randint(len(far))]
    return np.exp2(a.ravel()).repeat(32)


BF16 = ml_dtypes.bfloat16


def bf(x):
    return np.asarray(x, np.float32).astype(BF16)


def f64(x):
    return np.asarray(x).astype(np.float64)


B, N, C, F = 8, 32, 1024, 256
EPS_STD = 1e-5


def setup_inputs():
    u, s = mx_kscale(C), mx_kscale(C)
    rows = np.concatenate([u, u, s])
    return {"x": bf(np.random.standard_normal((B, N, C)) * u),
            "e_enc": bf(np.random.standard_normal((B, N, N, C)) * s),
            "W_pre": bf(np.random.standard_normal((3 * C, F)) / np.sqrt(3 * C) / rows[:, None]),
            "b_pre": bf(np.random.standard_normal(F) * 0.3)}


def reference(x, e_enc, W_pre, b_pre):
    w = f64(W_pre)
    xq = mxq(f64(x), 2, "e4m3")
    tgt = xq @ mxq(w[:C], 0, "e4m3")
    src = xq @ mxq(w[C:2 * C], 0, "e4m3")
    edg = mxq(f64(e_enc), 3, "e4m3") @ mxq(w[2 * C:], 0, "e4m3")
    m = tgt[:, :, None, :] + src[:, None, :, :] + edg + f64(b_pre)
    mean = m.mean(axis=2)
    mn = m.min(axis=2)
    mx = m.max(axis=2)
    var = (m * m).mean(axis=2) - mean * mean
    std = np.sqrt(np.maximum(var, 0.0) + EPS_STD)
    return np.concatenate([mean, mn, mx, std], axis=-1)

@@ -1,0 +1,380 @@
+from contextlib import ExitStack
+
+import concourse.mybir as mybir
+from concourse.masks import make_identity
+
+F32 = mybir.dt.float32
+BF16 = mybir.dt.bfloat16
+I32 = mybir.dt.int32
+U32 = mybir.dt.uint32
+U8 = mybir.dt.uint8
+FP8X4 = mybir.dt.float8_e4m3fn_x4
+ALU = mybir.AluOpType
+ACT = mybir.ActivationFunctionType
+AX = mybir.AxisListType
+
+P = 128
+B = 8
+N = 32
+C = 1024
+F = 256
+EPS_STD = 1e-5
+ROWS = 512
+NCH = B * N * N // ROWS
+TGT = ROWS // N
+FLOPS = 2 * C * F * (B * N * N + 2 * B * N)
+PRELOAD = 5
+SUMMED = NCH - 2
+
+
+def tile_gnnlayer_pa_t_kernel(tc, x, e_enc, W_pre, b_pre, out):
+    nc = tc.nc
+    with ExitStack() as ctx:
+        const = ctx.enter_context(tc.tile_pool(name="const", bufs=1))
+        epool = ctx.enter_context(tc.tile_pool(name="epool", bufs=6))
+        gpool = ctx.enter_context(tc.tile_pool(name="gpool", bufs=3))
+        qpool = ctx.enter_context(tc.tile_pool(name="qpool", bufs=3))
+        spool = ctx.enter_context(tc.tile_pool(name="spool", bufs=3))
+        tree = ctx.enter_context(tc.tile_pool(name="tree", bufs=2))
+        fpool = ctx.enter_context(tc.tile_pool(name="fpool", bufs=2))
+        tpsum = ctx.enter_context(tc.psum_pool(name="tpsum", bufs=4))
+        apsum = ctx.enter_context(tc.psum_pool(name="apsum", bufs=4))
+        ctx.enter_context(tc.manual_schedule())
+
+        eps_t = const.tile([P, 1], F32, name="eps_t")
+        warm = const.tile([P, 1], F32, name="warm")
+        ident = const.tile([P, P], F32, name="ident")
+        w_raw = const.tile([P, 6, 4, F], BF16, name="w_raw")
+        w_grp = const.tile([P, 6, F, 4], BF16, name="w_grp", align_bytes=64)
+        w_q = const.tile([P, 6, F], U32, name="w_q", align_bytes=64)
+        w_s = const.tile([P, 6, F], U8, name="w_s", align_bytes=64)
+        x_raw = const.tile([P, 2, C], BF16, name="x_raw")
+        x_grp = const.tile([P, 2, 2 * P, 2], F32, name="x_grp", align_bytes=64)
+        x_q = const.tile([P, 2, 2 * P], U32, name="x_q", align_bytes=64)
+        x_s = const.tile([P, 2, 2 * P], U8, name="x_s", align_bytes=64)
+        xr_q = const.tile([P, B, 2, P], U32, name="xr_q", align_bytes=64)
+        xr_s = const.tile([P, B, 2, P], U8, name="xr_s", align_bytes=64)
+        bias_bc = const.tile([P, F], BF16, name="bias_bc")
+        c_raw = const.tile([P, 2, F], F32, name="c_raw")
+        c_sb = const.tile([P, 2, F], F32, name="c_sb")
+        bst = const.tile([P, 2, B * N, 3], F32, name="bst")
+        s12 = const.tile([P, 2, B * N], F32, name="s12")
+        mins = const.tile([P, 2, B * N], F32, name="mins")
+        maxs = const.tile([P, 2, B * N], F32, name="maxs")
+
+        w_view = W_pre.rearrange("(s q t) c -> q s t c", q=P, t=4)
+        e_view = e_enc.flatten_outer_dims().rearrange("(c t p) k -> c p t k", t=4, p=P)
+        out_rows = out.flatten_outer_dims()
+
+        ets = {}
+        grps = {}
+        codes = {}
+        accs = {}
+        planes = {}
+        halves = {}
+        fin = {}
+
+        def load(c, pieces=1):
+            et = epool.tile([P, 4, C], BF16, name="et", tag="et")
+            step = 4 // pieces
+            for t in range(0, 4, step):
+                nc.sync.dma_start(out=et[:, t : t + step, :], in_=e_view[c][:, t : t + step, :])
+            ets[c] = et
+
+        def load_w(block):
+            nc.sync.dma_start(out=w_raw[:, 2 * block : 2 * block + 2], in_=w_view[:, 2 * block : 2 * block + 2])
+
+        def transpose_rows(rows):
+            tp = tpsum.tile([P, 4, P], F32, name="tp", tag="tp")
+            words = rows.bitcast(F32)
+            for a in range(4):
+                g, u = divmod(a, 2)
+                nc.tensor.transpose(tp[:, a, :], words[:, 2 * g * P + u : 2 * (g + 1) * P : 2], ident[:])
+            return tp
+
+        def evacuate(tp, dst):
+            nc.scalar.copy(out=dst, in_=tp[:].rearrange("p (g u) r -> p g r u", u=2))
+
+        def quantise(src, q_ap, s_ap):
+            nc.vector.quantize_mx(out=q_ap.bitcast(FP8X4), scales=s_ap, in_=src)
+
+        def quantise_w(block):
+            lo = 2 * block
+            quantise(
+                w_grp[:, lo : lo + 2].rearrange("p s c t -> p (s c t)"),
+                w_q[:, lo : lo + 2].rearrange("p s c -> p (s c)"),
+                w_s[:, lo : lo + 2].rearrange("p s c -> p (s c)"),
+            )
+
+        def regroup_views(s):
+            return (
+                w_grp[:, s].rearrange("p (c i) t -> p c t i", i=4),
+                w_raw[:, s].rearrange("p t (c i) -> p c t i", i=4),
+            )
+
+        def regroup_w_vector(block):
+            for s in (2 * block, 2 * block + 1):
+                dst, src = regroup_views(s)
+                nc.vector.tensor_copy(out=dst, in_=src)
+
+        def regroup_w_gpsimd(block):
+            for s in (2 * block, 2 * block + 1):
+                dst, src = regroup_views(s)
+                nc.gpsimd.tensor_scalar(out=dst, in0=src, scalar1=1.0, scalar2=0.0, op0=ALU.mult, op1=ALU.add)
+
+        def front(c):
+            grp = gpool.tile([P, 2, ROWS, 2], F32, name="grp", tag="grp", align_bytes=64)
+            for t in range(4):
+                tp = transpose_rows(ets[c][:, t, :])
+                evacuate(tp, grp[:, :, t * P : (t + 1) * P, :])
+            grps[c] = grp
+
+        def quantise_chunk(c):
+            eq = qpool.tile([P, 2, ROWS], U32, name="eq", tag="eq", align_bytes=64)
+            es = qpool.tile([P, 2, ROWS], U8, name="es", tag="es", align_bytes=64)
+            quantise(
+                grps[c][:].rearrange("p g n u -> p (g n u)").bitcast(BF16),
+                eq[:].rearrange("p g n -> p (g n)"),
+                es[:].rearrange("p g n -> p (g n)"),
+            )
+            codes[c] = (eq, es)
+
+        def mx(out_ap, s, cols, rhs, rhs_scale, start, stop):
+            nc.tensor.matmul_mx(
+                out=out_ap,
+                lhsT=w_q[:, s, cols].bitcast(FP8X4),
+                lhsT_scale=w_s[:, s, cols],
+                rhs=rhs.bitcast(FP8X4),
+                rhs_scale=rhs_scale,
+                start=start,
+                stop=stop,
+            )
+
+        def messages(c):
+            b = c // 2
+            eq, es = codes[c]
+            pair = {}
+            for ft in (1, 0):
+                cols = slice(ft * P, (ft + 1) * P)
+                acc = apsum.tile([P, ROWS], F32, name="acc", tag="acc")
+                mx(acc[:], 4, cols, eq[:, 0, :], es[:, 0, :], True, False)
+                for g in range(2):
+                    for q in range(4):
+                        mx(acc[:, q * P : (q + 1) * P], 2 + g, cols, xr_q[:, b, g, :], xr_s[:, b, g, :], False, False)
+                mx(acc[:], 5, cols, eq[:, 1, :], es[:, 1, :], False, True)
+                pair[ft] = acc
+                if ft == 1 and c < SUMMED:
+                    if c % 2 == 0:
+                        planes[c // 2] = spool.tile([P, 2, 2, ROWS], F32, name="pl", tag="pl")
+                    pl = planes[c // 2]
+                    nc.scalar.copy(out=pl[:, 0, c % 2, :], in_=acc[:])
+                    nc.scalar.activation(out=pl[:, 1, c % 2, :], in_=acc[:], func=ACT.Square)
+            accs[c] = pair
+
+        def reduces(c):
+            cols = slice(c * TGT, (c + 1) * TGT)
+            for ft in (1, 0):
+                m = accs[c][ft][:].rearrange("p (i j) -> p i j", j=N)
+                nc.vector.tensor_reduce(out=maxs[:, ft, cols], in_=m, axis=AX.X, op=ALU.max)
+                nc.vector.tensor_reduce(out=mins[:, ft, cols], in_=m, axis=AX.X, op=ALU.min)
+                if ft == 0 or c >= SUMMED:
+                    for i in range(0, TGT, 2):
+                        nc.vector.bn_stats(
+                            out=bst[:, ft, c * TGT + i : c * TGT + i + 2, :].rearrange("p m s -> p (m s)"),
+                            in_=m[:, i : i + 2, :].rearrange("p m j -> p j m"),
+                        )
+
+        def first_level(c):
+            if c % 2 == 0:
+                halves[c // 2] = tree.tile([P, 2, 2, TGT, N // 2], F32, name="lvl16", tag="lvl16")
+            src = planes[c // 2][:, :, c % 2, :].rearrange("p f (i j) -> p f i j", j=N)
+            nc.gpsimd.tensor_tensor(
+                out=halves[c // 2][:, :, c % 2, :, :], in0=src[:, :, :, 0 : N // 2], in1=src[:, :, :, N // 2 : N], op=ALU.add
+            )
+
+        def upper_levels(pair):
+            cols = slice(2 * pair * TGT, 2 * (pair + 1) * TGT)
+            cur = halves[pair][:].rearrange("p f c i j -> p (f c i) j")
+            for width in (8, 4, 2):
+                nxt = tree.tile([P, 4 * TGT, width], F32, name="lvl%d" % width, tag="lvl%d" % width)
+                nc.gpsimd.tensor_tensor(out=nxt[:], in0=cur[:, :, 0:width], in1=cur[:, :, width : 2 * width], op=ALU.add)
+                cur = nxt[:]
+            last = cur.rearrange("p (f i) j -> p f i j", f=2)
+            nc.gpsimd.tensor_tensor(out=s12[:, :, cols], in0=last[:, :, :, 0], in1=last[:, :, :, 1], op=ALU.add)
+
+        def target_term():
+            tg = tpsum.tile([P, 2, F], F32, name="tg", tag="tp")
+            for hb in range(2):
+                for g in range(2):
+                    nc.tensor.matmul_mx(
+                        out=tg[:, hb, :],
+                        lhsT=x_q[:, g, hb * P : (hb + 1) * P].bitcast(FP8X4),
+                        lhsT_scale=x_s[:, g, hb * P : (hb + 1) * P],
+                        rhs=w_q[:, g, :].bitcast(FP8X4),
+                        rhs_scale=w_s[:, g, :],
+                        start=(g == 0),
+                        stop=(g == 1),
+                    )
+            nc.scalar.copy(out=c_raw[:], in_=tg[:])
+
+        def target_bias():
+            nc.gpsimd.tensor_tensor(
+                out=c_sb[:], in0=c_raw[:], in1=bias_bc[:].unsqueeze(1).to_broadcast([P, 2, F]), op=ALU.add
+            )
+
+        def finish_tiles(hb):
+            fin[hb] = {
+                "mean": fpool.tile([P, 2, P], F32, name="mean", tag="mean"),
+                "var": fpool.tile([P, 2, P], F32, name="var", tag="var"),
+                "msq": fpool.tile([P, P], F32, name="msq", tag="msq"),
+            }
+
+        def means_of_summed(hb, width):
+            cols = slice(hb * P, hb * P + width)
+            nc.scalar.copy(out=fin[hb]["mean"][:, 0, 0:width], in_=bst[:, 0, cols, 1])
+            nc.scalar.mul(out=fin[hb]["mean"][:, 1, 0:width], in_=s12[:, 0, cols], mul=1.0 / N)
+            nc.scalar.activation(out=fin[hb]["msq"][:, 0:width], in_=s12[:, 0, cols], func=ACT.Square, scale=1.0 / N)
+
+        def variances_of_summed(hb, width):
+            cols = slice(hb * P, hb * P + width)
+            nc.vector.tensor_scalar_mul(out=fin[hb]["var"][:, 0, 0:width], in0=bst[:, 0, cols, 2], scalar1=1.0 / N)
+            nc.vector.scalar_tensor_tensor(
+                out=fin[hb]["var"][:, 1, 0:width],
+                in0=s12[:, 1, cols],
+                scalar=1.0 / N,
+                in1=fin[hb]["msq"][:, 0:width],
+                op0=ALU.mult,
+                op1=ALU.subtract,
+            )
+
+        def variances_of_rest(hb, width):
+            if width < P:
+                cols = slice(hb * P + width, (hb + 1) * P)
+                nc.vector.tensor_scalar_mul(out=fin[hb]["var"][:, :, width:P], in0=bst[:, :, cols, 2], scalar1=1.0 / N)
+            nc.vector.tensor_scalar_max(out=fin[hb]["var"][:], in0=fin[hb]["var"][:], scalar1=0.0)
+
+        def means_of_rest(hb, width):
+            cols = slice(hb * P + width, (hb + 1) * P)
+            nc.vector.tensor_copy(out=fin[hb]["mean"][:, :, width:P], in_=bst[:, :, cols, 1])
+
+        def finish_transposes(hb):
+            cols = slice(hb * P, (hb + 1) * P)
+            fv = tpsum.tile([P, 2, P], F32, name="fv", tag="tp")
+            fx = tpsum.tile([P, 2, P], F32, name="fx", tag="tp")
+            fm = tpsum.tile([P, 4, P], F32, name="fm", tag="tp")
+            for ft in range(2):
+                nc.tensor.transpose(fv[:, ft, :], fin[hb]["var"][:, ft, :], ident[:])
+            for ft in range(2):
+                nc.tensor.transpose(fx[:, ft, :], maxs[:, ft, cols], ident[:])
+            for ft in range(2):
+                nc.tensor.transpose(fm[:, ft, :], fin[hb]["mean"][:, ft, :], ident[:])
+            for ft in range(2):
+                nc.tensor.transpose(fm[:, 2 + ft, :], mins[:, ft, cols], ident[:])
+            fin[hb]["fv"] = fv
+            fin[hb]["fx"] = fx
+            fin[hb]["fm"] = fm
+
+        def finish_stores(hb):
+            rows = slice(hb * P, (hb + 1) * P)
+            hi = fpool.tile([P, 2, F], F32, name="hi", tag="hi")
+            lo = fpool.tile([P, 2, F], F32, name="lo", tag="lo")
+            nc.scalar.activation(
+                out=hi[:, 1, :], in_=fin[hb]["fv"][:].rearrange("p f r -> p (f r)"), func=ACT.Sqrt, bias=eps_t[:]
+            )
+            nc.vector.tensor_tensor(
+                out=hi[:, 0, :], in0=fin[hb]["fx"][:].rearrange("p f r -> p (f r)"), in1=c_sb[:, hb, :], op=ALU.add
+            )
+            nc.sync.dma_start(out=out_rows[rows, 2 * F : 4 * F], in_=hi[:].rearrange("p s f -> p (s f)"))
+            nc.vector.tensor_tensor(
+                out=lo[:],
+                in0=fin[hb]["fm"][:].rearrange("p (s f) r -> p s (f r)", f=2),
+                in1=c_sb[:, hb, :].unsqueeze(1).to_broadcast([P, 2, F]),
+                op=ALU.add,
+            )
+            nc.sync.dma_start(out=out_rows[rows, 0 : 2 * F], in_=lo[:].rearrange("p s f -> p (s f)"))
+
+        def repeat_sources(b0, b1):
+            for g in range(2):
+                nc.vector.tensor_copy(
+                    out=xr_q[:, b0:b1, g, :].bitcast(I32).rearrange("p b (d j) -> p b d j", d=4),
+                    in_=x_q[:, g, b0 * N : b1 * N].bitcast(I32).rearrange("p (b j) -> p b j", j=N).unsqueeze(2).to_broadcast([P, b1 - b0, 4, N]),
+                )
+                nc.vector.tensor_copy(
+                    out=xr_s[:, b0:b1, g, :].bitcast(I32).rearrange("p b (d j) -> p b d j", d=4),
+                    in_=x_s[:, g, b0 * N : b1 * N].bitcast(I32).rearrange("p (b j) -> p b j", j=N // 4).unsqueeze(2).to_broadcast([P, b1 - b0, 4, N // 4]),
+                )
+
+        nc.sync.dma_start(out=x_raw[:], in_=x.flatten_outer_dims().rearrange("(t p) k -> p t k", p=P))
+        load(0, 4)
+        load_w(2)
+        load_w(1)
+        load(1)
+        load(2)
+        load_w(0)
+        nc.sync.dma_start(out=bias_bc[:], in_=b_pre.partition_broadcast(P))
+        load(3)
+        load(4)
+
+        nc.vector.memset(eps_t[:], EPS_STD)
+        nc.vector.memset(warm[:], 1.0)
+        nc.vector.memset(x_s[:].rearrange("p g n -> p (g n)").bitcast(I32), 0)
+        nc.scalar.sqrt(warm[:], warm[:])
+        make_identity(nc, ident[:])
+        regroup_w_gpsimd(0)
+
+        for t in range(2):
+            tp = transpose_rows(x_raw[:, t, :])
+            evacuate(tp, x_grp[:, :, t * P : (t + 1) * P, :])
+        quantise(
+            x_grp[:].rearrange("p g n u -> p (g n u)").bitcast(BF16),
+            x_q[:].rearrange("p g n -> p (g n)"),
+            x_s[:].rearrange("p g n -> p (g n)"),
+        )
+        repeat_sources(0, 1)
+        regroup_w_vector(2)
+        quantise_w(2)
+
+        LAST = P - 2 * TGT
+        for n in range(-2, NCH + 1):
+            if 0 <= n and n + PRELOAD < NCH:
+                load(n + PRELOAD)
+            if n == 11:
+                finish_tiles(0)
+                means_of_summed(0, P)
+            if n + 2 < NCH:
+                front(n + 2)
+            if n == 13:
+                finish_transposes(0)
+            if 0 <= n < NCH:
+                messages(n)
+            if n == 4:
+                target_term()
+            if n == 12:
+                variances_of_summed(0, P)
+                variances_of_rest(0, P)
+            if n == 14:
+                finish_stores(0)
+            if n == 3:
+                quantise_w(0)
+            if 0 <= n + 1 < NCH:
+                quantise_chunk(n + 1)
+            if n == -1:
+                regroup_w_vector(1)
+                quantise_w(1)
+                repeat_sources(1, B)
+            if n == 16:
+                finish_tiles(1)
+                means_of_summed(1, LAST)
+                variances_of_summed(1, LAST)
+            if n >= 1:
+                reduces(n - 1)
+                if n - 1 < SUMMED:
+                    first_level(n - 1)
+                    if (n - 1) % 2 == 1:
+                        upper_levels((n - 1) // 2)
+            if n == 6:
+                target_bias()
+        variances_of_rest(1, LAST)
+        means_of_rest(1, LAST)
+        finish_transposes(1)
+        finish_stores(1)

@@ -22,16 +22,18 @@ EPS_STD = 1e-5
 ROWS = 512
 NCH = B * N * N // ROWS
 TGT = ROWS // N
+REP = 8
 FLOPS = 2 * C * F * (B * N * N + 2 * B * N)
-PRELOAD = 5
-SUMMED = NCH - 2
+PRELOAD = 4
+SUMMED = NCH - 1
 
 
 def tile_gnnlayer_pa_t_kernel(tc, x, e_enc, W_pre, b_pre, out):
     nc = tc.nc
     with ExitStack() as ctx:
         const = ctx.enter_context(tc.tile_pool(name="const", bufs=1))
-        epool = ctx.enter_context(tc.tile_pool(name="epool", bufs=6))
+        epool = ctx.enter_context(tc.tile_pool(name="epool", bufs=5))
+        ppool = ctx.enter_context(tc.tile_pool(name="ppool", bufs=2))
         gpool = ctx.enter_context(tc.tile_pool(name="gpool", bufs=3))
         qpool = ctx.enter_context(tc.tile_pool(name="qpool", bufs=3))
         spool = ctx.enter_context(tc.tile_pool(name="spool", bufs=3))
@@ -49,11 +51,11 @@ def tile_gnnlayer_pa_t_kernel(tc, x, e_enc, W_pre, b_pre, out):
         w_q = const.tile([P, 6, F], U32, name="w_q", align_bytes=64)
         w_s = const.tile([P, 6, F], U8, name="w_s", align_bytes=64)
         x_raw = const.tile([P, 2, C], BF16, name="x_raw")
-        x_grp = const.tile([P, 2, 2 * P, 2], F32, name="x_grp", align_bytes=64)
-        x_q = const.tile([P, 2, 2 * P], U32, name="x_q", align_bytes=64)
-        x_s = const.tile([P, 2, 2 * P], U8, name="x_s", align_bytes=64)
-        xr_q = const.tile([P, B, 2, P], U32, name="xr_q", align_bytes=64)
-        xr_s = const.tile([P, B, 2, P], U8, name="xr_s", align_bytes=64)
+        x_grp = const.tile([P, 2, 2, P, 2], F32, name="x_grp", align_bytes=64)
+        x_q = const.tile([P, 2, 2, P], U32, name="x_q", align_bytes=64)
+        x_s = const.tile([P, 2, 2, P], U8, name="x_s", align_bytes=64)
+        xr_q = const.tile([P, B, 2, REP * N], U32, name="xr_q", align_bytes=64)
+        xr_s = const.tile([P, B, 2, REP * N], U8, name="xr_s", align_bytes=64)
         bias_bc = const.tile([P, F], BF16, name="bias_bc")
         c_raw = const.tile([P, 2, F], F32, name="c_raw")
         c_sb = const.tile([P, 2, F], F32, name="c_sb")
@@ -63,10 +65,12 @@ def tile_gnnlayer_pa_t_kernel(tc, x, e_enc, W_pre, b_pre, out):
         maxs = const.tile([P, 2, B * N], F32, name="maxs")
 
         w_view = W_pre.rearrange("(s q t) c -> q s t c", q=P, t=4)
+        x_view = x.flatten_outer_dims().rearrange("(t p) k -> p t k", p=P)
         e_view = e_enc.flatten_outer_dims().rearrange("(c t p) k -> c p t k", t=4, p=P)
         out_rows = out.flatten_outer_dims()
 
         ets = {}
+        perms = {}
         grps = {}
         codes = {}
         accs = {}
@@ -84,12 +88,21 @@ def tile_gnnlayer_pa_t_kernel(tc, x, e_enc, W_pre, b_pre, out):
         def load_w(block):
             nc.sync.dma_start(out=w_raw[:, 2 * block : 2 * block + 2], in_=w_view[:, 2 * block : 2 * block + 2])
 
+        def load_x(t):
+            nc.sync.dma_start(out=x_raw[:, t, :], in_=x_view[:, t, :])
+
         def transpose_rows(rows):
             tp = tpsum.tile([P, 4, P], F32, name="tp", tag="tp")
             words = rows.bitcast(F32)
             for a in range(4):
                 g, u = divmod(a, 2)
                 nc.tensor.transpose(tp[:, a, :], words[:, 2 * g * P + u : 2 * (g + 1) * P : 2], ident[:])
+            return tp
+
+        def transpose_permuted(perm):
+            tp = tpsum.tile([P, 4, P], F32, name="tp", tag="tp")
+            for a in range(4):
+                nc.tensor.transpose(tp[:, a, :], perm[:, a, :], ident[:])
             return tp
 
         def evacuate(tp, dst):
@@ -112,20 +125,47 @@ def tile_gnnlayer_pa_t_kernel(tc, x, e_enc, W_pre, b_pre, out):
                 w_raw[:, s].rearrange("p t (c i) -> p c t i", i=4),
             )
 
-        def regroup_w_vector(block):
-            for s in (2 * block, 2 * block + 1):
-                dst, src = regroup_views(s)
-                nc.vector.tensor_copy(out=dst, in_=src)
+        def regroup_w_vector(s):
+            dst, src = regroup_views(s)
+            nc.vector.tensor_copy(out=dst, in_=src)
 
-        def regroup_w_gpsimd(block):
-            for s in (2 * block, 2 * block + 1):
-                dst, src = regroup_views(s)
-                nc.gpsimd.tensor_scalar(out=dst, in0=src, scalar1=1.0, scalar2=0.0, op0=ALU.mult, op1=ALU.add)
+        def regroup_w_scalar(s):
+            dst, src = regroup_views(s)
+            nc.scalar.copy(out=dst, in_=src)
+
+        def front_x(t):
+            evacuate(transpose_rows(x_raw[:, t, :]), x_grp[:, t])
+
+        def quantise_x(t):
+            quantise(
+                x_grp[:, t].rearrange("p g n u -> p (g n u)").bitcast(BF16),
+                x_q[:, t].rearrange("p g n -> p (g n)"),
+                x_s[:, t].rearrange("p g n -> p (g n)"),
+            )
+
+        def repeat_sources(b):
+            t, lo = divmod(b * N, P)
+            nc.vector.tensor_copy(
+                out=xr_q[:, b].bitcast(I32).rearrange("p g (d j) -> p g d j", d=REP),
+                in_=x_q[:, t, :, lo : lo + N].bitcast(I32).unsqueeze(2).to_broadcast([P, 2, REP, N]),
+            )
+            nc.vector.tensor_copy(
+                out=xr_s[:, b].bitcast(I32).rearrange("p g (d j) -> p g d j", d=REP),
+                in_=x_s[:, t, :, lo : lo + N].bitcast(I32).unsqueeze(2).to_broadcast([P, 2, REP, N // 4]),
+            )
+
+        def permute(c):
+            perm = ppool.tile([P, 4, P], F32, name="perm", tag="perm")
+            nc.scalar.copy(
+                out=perm[:].rearrange("p (g u) w -> p g u w", u=2),
+                in_=ets[c][:, 3, :].bitcast(F32).rearrange("p (g w u) -> p g u w", g=2, u=2),
+            )
+            perms[c] = perm
 
         def front(c):
             grp = gpool.tile([P, 2, ROWS, 2], F32, name="grp", tag="grp", align_bytes=64)
             for t in range(4):
-                tp = transpose_rows(ets[c][:, t, :])
+                tp = transpose_permuted(perms[c]) if t == 3 and c in perms else transpose_rows(ets[c][:, t, :])
                 evacuate(tp, grp[:, :, t * P : (t + 1) * P, :])
             grps[c] = grp
 
@@ -159,30 +199,40 @@ def tile_gnnlayer_pa_t_kernel(tc, x, e_enc, W_pre, b_pre, out):
                 acc = apsum.tile([P, ROWS], F32, name="acc", tag="acc")
                 mx(acc[:], 4, cols, eq[:, 0, :], es[:, 0, :], True, False)
                 for g in range(2):
-                    for q in range(4):
-                        mx(acc[:, q * P : (q + 1) * P], 2 + g, cols, xr_q[:, b, g, :], xr_s[:, b, g, :], False, False)
+                    for lo in range(0, ROWS, REP * N):
+                        mx(acc[:, lo : lo + REP * N], 2 + g, cols, xr_q[:, b, g, :], xr_s[:, b, g, :], False, False)
                 mx(acc[:], 5, cols, eq[:, 1, :], es[:, 1, :], False, True)
                 pair[ft] = acc
-                if ft == 1 and c < SUMMED:
-                    if c % 2 == 0:
-                        planes[c // 2] = spool.tile([P, 2, 2, ROWS], F32, name="pl", tag="pl")
-                    pl = planes[c // 2]
-                    nc.scalar.copy(out=pl[:, 0, c % 2, :], in_=acc[:])
-                    nc.scalar.activation(out=pl[:, 1, c % 2, :], in_=acc[:], func=ACT.Square)
             accs[c] = pair
 
-        def reduces(c):
-            cols = slice(c * TGT, (c + 1) * TGT)
-            for ft in (1, 0):
-                m = accs[c][ft][:].rearrange("p (i j) -> p i j", j=N)
-                nc.vector.tensor_reduce(out=maxs[:, ft, cols], in_=m, axis=AX.X, op=ALU.max)
-                nc.vector.tensor_reduce(out=mins[:, ft, cols], in_=m, axis=AX.X, op=ALU.min)
-                if ft == 0 or c >= SUMMED:
-                    for i in range(0, TGT, 2):
-                        nc.vector.bn_stats(
-                            out=bst[:, ft, c * TGT + i : c * TGT + i + 2, :].rearrange("p m s -> p (m s)"),
-                            in_=m[:, i : i + 2, :].rearrange("p m j -> p j m"),
-                        )
+        def copies(c):
+            if c % 2 == 0:
+                planes[c // 2] = spool.tile([P, 2, 2, ROWS], F32, name="pl", tag="pl")
+            pl = planes[c // 2]
+            nc.scalar.copy(out=pl[:, 0, c % 2, :], in_=accs[c][1][:])
+            nc.scalar.activation(out=pl[:, 1, c % 2, :], in_=accs[c][1][:], func=ACT.Square)
+
+        def extremes(c, ft, op, dst):
+            nc.vector.tensor_reduce(
+                out=dst[:, ft, c * TGT : (c + 1) * TGT],
+                in_=accs[c][ft][:].rearrange("p (i j) -> p i j", j=N),
+                axis=AX.X,
+                op=op,
+            )
+
+        def sums(c, ft):
+            m = accs[c][ft][:].rearrange("p (i j) -> p i j", j=N)
+            for i in range(0, TGT, 2):
+                nc.vector.bn_stats(
+                    out=bst[:, ft, c * TGT + i : c * TGT + i + 2, :].rearrange("p m s -> p (m s)"),
+                    in_=m[:, i : i + 2, :].rearrange("p m j -> p j m"),
+                )
+
+        def reduces(c, ft):
+            extremes(c, ft, ALU.max, maxs)
+            extremes(c, ft, ALU.min, mins)
+            if ft == 0:
+                sums(c, 0)
 
         def first_level(c):
             if c % 2 == 0:
@@ -192,15 +242,15 @@ def tile_gnnlayer_pa_t_kernel(tc, x, e_enc, W_pre, b_pre, out):
                 out=halves[c // 2][:, :, c % 2, :, :], in0=src[:, :, :, 0 : N // 2], in1=src[:, :, :, N // 2 : N], op=ALU.add
             )
 
-        def upper_levels(pair):
-            cols = slice(2 * pair * TGT, 2 * (pair + 1) * TGT)
-            cur = halves[pair][:].rearrange("p f c i j -> p (f c i) j")
+        def upper_levels(c, count):
+            cols = slice((c + 1 - count) * TGT, (c + 1) * TGT)
+            rows = count * TGT
+            cur = halves[c // 2][:, :, 0:count].rearrange("p f c i j -> p f (c i) j")
             for width in (8, 4, 2):
-                nxt = tree.tile([P, 4 * TGT, width], F32, name="lvl%d" % width, tag="lvl%d" % width)
-                nc.gpsimd.tensor_tensor(out=nxt[:], in0=cur[:, :, 0:width], in1=cur[:, :, width : 2 * width], op=ALU.add)
+                nxt = tree.tile([P, 2, rows, width], F32, name="lvl%d_%d" % (width, count), tag="lvl%d_%d" % (width, count))
+                nc.gpsimd.tensor_tensor(out=nxt[:], in0=cur[:, :, :, 0:width], in1=cur[:, :, :, width : 2 * width], op=ALU.add)
                 cur = nxt[:]
-            last = cur.rearrange("p (f i) j -> p f i j", f=2)
-            nc.gpsimd.tensor_tensor(out=s12[:, :, cols], in0=last[:, :, :, 0], in1=last[:, :, :, 1], op=ALU.add)
+            nc.gpsimd.tensor_tensor(out=s12[:, :, cols], in0=cur[:, :, :, 0], in1=cur[:, :, :, 1], op=ALU.add)
 
         def target_term():
             tg = tpsum.tile([P, 2, F], F32, name="tg", tag="tp")
@@ -208,8 +258,8 @@ def tile_gnnlayer_pa_t_kernel(tc, x, e_enc, W_pre, b_pre, out):
                 for g in range(2):
                     nc.tensor.matmul_mx(
                         out=tg[:, hb, :],
-                        lhsT=x_q[:, g, hb * P : (hb + 1) * P].bitcast(FP8X4),
-                        lhsT_scale=x_s[:, g, hb * P : (hb + 1) * P],
+                        lhsT=x_q[:, hb, g, :].bitcast(FP8X4),
+                        lhsT_scale=x_s[:, hb, g, :],
                         rhs=w_q[:, g, :].bitcast(FP8X4),
                         rhs_scale=w_s[:, g, :],
                         start=(g == 0),
@@ -224,20 +274,22 @@ def tile_gnnlayer_pa_t_kernel(tc, x, e_enc, W_pre, b_pre, out):
 
         def finish_tiles(hb):
             fin[hb] = {
-                "mean": fpool.tile([P, 2, P], F32, name="mean", tag="mean"),
+                "mean": fpool.tile([P, P], F32, name="mean", tag="mean"),
                 "var": fpool.tile([P, 2, P], F32, name="var", tag="var"),
                 "msq": fpool.tile([P, P], F32, name="msq", tag="msq"),
+                "res": fpool.tile([P, 4, F], F32, name="res", tag="res"),
             }
 
         def means_of_summed(hb, width):
             cols = slice(hb * P, hb * P + width)
-            nc.scalar.copy(out=fin[hb]["mean"][:, 0, 0:width], in_=bst[:, 0, cols, 1])
-            nc.scalar.mul(out=fin[hb]["mean"][:, 1, 0:width], in_=s12[:, 0, cols], mul=1.0 / N)
+            nc.scalar.mul(out=fin[hb]["mean"][:, 0:width], in_=s12[:, 0, cols], mul=1.0 / N)
             nc.scalar.activation(out=fin[hb]["msq"][:, 0:width], in_=s12[:, 0, cols], func=ACT.Square, scale=1.0 / N)
 
         def variances_of_summed(hb, width):
             cols = slice(hb * P, hb * P + width)
-            nc.vector.tensor_scalar_mul(out=fin[hb]["var"][:, 0, 0:width], in0=bst[:, 0, cols, 2], scalar1=1.0 / N)
+            nc.vector.tensor_scalar(
+                out=fin[hb]["var"][:, 0, 0:width], in0=bst[:, 0, cols, 2], scalar1=1.0 / N, scalar2=0.0, op0=ALU.mult, op1=ALU.max
+            )
             nc.vector.scalar_tensor_tensor(
                 out=fin[hb]["var"][:, 1, 0:width],
                 in0=s12[:, 1, cols],
@@ -247,134 +299,148 @@ def tile_gnnlayer_pa_t_kernel(tc, x, e_enc, W_pre, b_pre, out):
                 op1=ALU.subtract,
             )
 
-        def variances_of_rest(hb, width):
-            if width < P:
-                cols = slice(hb * P + width, (hb + 1) * P)
-                nc.vector.tensor_scalar_mul(out=fin[hb]["var"][:, :, width:P], in0=bst[:, :, cols, 2], scalar1=1.0 / N)
-            nc.vector.tensor_scalar_max(out=fin[hb]["var"][:], in0=fin[hb]["var"][:], scalar1=0.0)
+        def clamp_summed(hb, width):
+            nc.vector.tensor_scalar_max(out=fin[hb]["var"][:, 1, 0:width], in0=fin[hb]["var"][:, 1, 0:width], scalar1=0.0)
 
-        def means_of_rest(hb, width):
+        def rest(hb, width):
             cols = slice(hb * P + width, (hb + 1) * P)
-            nc.vector.tensor_copy(out=fin[hb]["mean"][:, :, width:P], in_=bst[:, :, cols, 1])
+            nc.vector.tensor_scalar(
+                out=fin[hb]["var"][:, :, width:P], in0=bst[:, :, cols, 2], scalar1=1.0 / N, scalar2=0.0, op0=ALU.mult, op1=ALU.max
+            )
+            nc.scalar.copy(out=fin[hb]["mean"][:, width:P], in_=bst[:, 1, cols, 1])
 
-        def finish_transposes(hb):
-            cols = slice(hb * P, (hb + 1) * P)
-            fv = tpsum.tile([P, 2, P], F32, name="fv", tag="tp")
-            fx = tpsum.tile([P, 2, P], F32, name="fx", tag="tp")
-            fm = tpsum.tile([P, 4, P], F32, name="fm", tag="tp")
+        def turn(name, planes2):
+            tp = tpsum.tile([P, 2, P], F32, name=name, tag="tp")
             for ft in range(2):
-                nc.tensor.transpose(fv[:, ft, :], fin[hb]["var"][:, ft, :], ident[:])
-            for ft in range(2):
-                nc.tensor.transpose(fx[:, ft, :], maxs[:, ft, cols], ident[:])
-            for ft in range(2):
-                nc.tensor.transpose(fm[:, ft, :], fin[hb]["mean"][:, ft, :], ident[:])
-            for ft in range(2):
-                nc.tensor.transpose(fm[:, 2 + ft, :], mins[:, ft, cols], ident[:])
-            fin[hb]["fv"] = fv
-            fin[hb]["fx"] = fx
-            fin[hb]["fm"] = fm
+                nc.tensor.transpose(tp[:, ft, :], planes2[ft], ident[:])
+            return tp[:].rearrange("p f r -> p (f r)")
 
-        def finish_stores(hb):
+        def store(hb, slots):
             rows = slice(hb * P, (hb + 1) * P)
-            hi = fpool.tile([P, 2, F], F32, name="hi", tag="hi")
-            lo = fpool.tile([P, 2, F], F32, name="lo", tag="lo")
-            nc.scalar.activation(
-                out=hi[:, 1, :], in_=fin[hb]["fv"][:].rearrange("p f r -> p (f r)"), func=ACT.Sqrt, bias=eps_t[:]
+            nc.sync.dma_start(
+                out=out_rows[rows, slots.start * F : slots.stop * F],
+                in_=fin[hb]["res"][:, slots].rearrange("p s f -> p (s f)"),
             )
-            nc.vector.tensor_tensor(
-                out=hi[:, 0, :], in0=fin[hb]["fx"][:].rearrange("p f r -> p (f r)"), in1=c_sb[:, hb, :], op=ALU.add
-            )
-            nc.sync.dma_start(out=out_rows[rows, 2 * F : 4 * F], in_=hi[:].rearrange("p s f -> p (s f)"))
-            nc.vector.tensor_tensor(
-                out=lo[:],
-                in0=fin[hb]["fm"][:].rearrange("p (s f) r -> p s (f r)", f=2),
-                in1=c_sb[:, hb, :].unsqueeze(1).to_broadcast([P, 2, F]),
-                op=ALU.add,
-            )
-            nc.sync.dma_start(out=out_rows[rows, 0 : 2 * F], in_=lo[:].rearrange("p s f -> p (s f)"))
 
-        def repeat_sources(b0, b1):
-            for g in range(2):
-                nc.vector.tensor_copy(
-                    out=xr_q[:, b0:b1, g, :].bitcast(I32).rearrange("p b (d j) -> p b d j", d=4),
-                    in_=x_q[:, g, b0 * N : b1 * N].bitcast(I32).rearrange("p (b j) -> p b j", j=N).unsqueeze(2).to_broadcast([P, b1 - b0, 4, N]),
-                )
-                nc.vector.tensor_copy(
-                    out=xr_s[:, b0:b1, g, :].bitcast(I32).rearrange("p b (d j) -> p b d j", d=4),
-                    in_=x_s[:, g, b0 * N : b1 * N].bitcast(I32).rearrange("p (b j) -> p b j", j=N // 4).unsqueeze(2).to_broadcast([P, b1 - b0, 4, N // 4]),
-                )
+        def finish_std(hb):
+            fv = turn("fv", [fin[hb]["var"][:, 0, :], fin[hb]["var"][:, 1, :]])
+            nc.scalar.activation(out=fin[hb]["res"][:, 3, :], in_=fv, func=ACT.Sqrt, bias=eps_t[:])
 
-        nc.sync.dma_start(out=x_raw[:], in_=x.flatten_outer_dims().rearrange("(t p) k -> p t k", p=P))
-        load(0, 4)
+        def turn_means(hb):
+            fin[hb]["t0"] = turn("fm", [bst[:, 0, hb * P : (hb + 1) * P, 1], fin[hb]["mean"][:]])
+
+        def turn_extremes(hb, slot, src):
+            fin[hb]["t%d" % slot] = turn("fx", [src[:, ft, hb * P : (hb + 1) * P] for ft in range(2)])
+
+        def add_target(hb, slot):
+            nc.vector.tensor_tensor(out=fin[hb]["res"][:, slot, :], in0=fin[hb]["t%d" % slot], in1=c_sb[:, hb, :], op=ALU.add)
+
         load_w(2)
-        load_w(1)
+        load(0, 4)
+        nc.sync.dma_start(out=x_raw[:, 0, :], in_=x_view[:, 0, :])
         load(1)
+        load_w(1)
         load(2)
+        load(3)
+        nc.sync.dma_start(out=x_raw[:, 1, :], in_=x_view[:, 1, :])
         load_w(0)
         nc.sync.dma_start(out=bias_bc[:], in_=b_pre.partition_broadcast(P))
-        load(3)
-        load(4)
 
         nc.vector.memset(eps_t[:], EPS_STD)
         nc.vector.memset(warm[:], 1.0)
-        nc.vector.memset(x_s[:].rearrange("p g n -> p (g n)").bitcast(I32), 0)
+        nc.vector.memset(x_s[:].rearrange("p t g n -> p (t g n)").bitcast(I32), 0)
         nc.scalar.sqrt(warm[:], warm[:])
         make_identity(nc, ident[:])
-        regroup_w_gpsimd(0)
 
-        for t in range(2):
-            tp = transpose_rows(x_raw[:, t, :])
-            evacuate(tp, x_grp[:, :, t * P : (t + 1) * P, :])
-        quantise(
-            x_grp[:].rearrange("p g n u -> p (g n u)").bitcast(BF16),
-            x_q[:].rearrange("p g n -> p (g n)"),
-            x_s[:].rearrange("p g n -> p (g n)"),
-        )
-        repeat_sources(0, 1)
-        regroup_w_vector(2)
+        front(0)
+        front_x(0)
+        regroup_w_vector(4)
+        regroup_w_vector(5)
         quantise_w(2)
+        quantise_chunk(0)
+        front(1)
+        quantise_x(0)
+        regroup_w_vector(2)
+        regroup_w_vector(3)
+        repeat_sources(0)
+        quantise_w(1)
 
-        LAST = P - 2 * TGT
-        for n in range(-2, NCH + 1):
-            if 0 <= n and n + PRELOAD < NCH:
+        LAST = P - TGT
+        for n in range(0, NCH + 1):
+            if n + PRELOAD < NCH:
                 load(n + PRELOAD)
-            if n == 11:
-                finish_tiles(0)
-                means_of_summed(0, P)
+            if n + 2 < NCH:
+                permute(n + 2)
+            if n < NCH:
+                messages(n)
+            if n == 8:
+                target_term()
+            if n < SUMMED:
+                copies(n)
+            if n == 4:
+                front_x(1)
             if n + 2 < NCH:
                 front(n + 2)
-            if n == 13:
-                finish_transposes(0)
-            if 0 <= n < NCH:
-                messages(n)
-            if n == 4:
-                target_term()
-            if n == 12:
-                variances_of_summed(0, P)
-                variances_of_rest(0, P)
-            if n == 14:
-                finish_stores(0)
             if n == 3:
-                quantise_w(0)
-            if 0 <= n + 1 < NCH:
+                regroup_w_scalar(0)
+            if n == 4:
+                regroup_w_scalar(1)
+            if n == 9:
+                finish_tiles(0)
+                means_of_summed(0, P)
+            if 1 <= n < NCH:
+                reduces(n - 1, 1)
+            if n + 1 < NCH:
                 quantise_chunk(n + 1)
-            if n == -1:
-                regroup_w_vector(1)
-                quantise_w(1)
-                repeat_sources(1, B)
-            if n == 16:
+            if 1 <= n < NCH:
+                reduces(n - 1, 0)
+            if n == 5:
+                quantise_x(1)
+            if n == 6:
+                quantise_w(0)
+            if n % 2 == 0 and n // 2 + 1 < B:
+                repeat_sources(n // 2 + 1)
+            if n < SUMMED:
+                first_level(n)
+                if n % 2 == 1:
+                    upper_levels(n, 2)
+                if n == SUMMED - 1:
+                    upper_levels(n, 1)
+            if n == 9:
+                target_bias()
+            if n == 10:
+                variances_of_summed(0, P)
+            if n == 11:
+                clamp_summed(0, P)
+            if n == 12:
+                finish_std(0)
+                turn_means(0)
+                turn_extremes(0, 2, maxs)
+                turn_extremes(0, 1, mins)
+            if n == 13:
+                for slot in (0, 2, 1):
+                    add_target(0, slot)
+                store(0, slice(0, 4))
+            if n == NCH - 1:
                 finish_tiles(1)
                 means_of_summed(1, LAST)
                 variances_of_summed(1, LAST)
-            if n >= 1:
-                reduces(n - 1)
-                if n - 1 < SUMMED:
-                    first_level(n - 1)
-                    if (n - 1) % 2 == 1:
-                        upper_levels((n - 1) // 2)
-            if n == 6:
-                target_bias()
-        variances_of_rest(1, LAST)
-        means_of_rest(1, LAST)
-        finish_transposes(1)
-        finish_stores(1)
+        c = NCH - 1
+        extremes(c, 1, ALU.max, maxs)
+        sums(c, 1)
+        extremes(c, 1, ALU.min, mins)
+        clamp_summed(1, LAST)
+        sums(c, 0)
+        extremes(c, 0, ALU.max, maxs)
+        rest(1, LAST)
+        finish_std(1)
+        turn_means(1)
+        turn_extremes(1, 2, maxs)
+        store(1, slice(3, 4))
+        extremes(c, 0, ALU.min, mins)
+        turn_extremes(1, 1, mins)
+        add_target(1, 0)
+        add_target(1, 2)
+        add_target(1, 1)
+        store(1, slice(2, 3))
+        store(1, slice(0, 2))

@@ -22,10 +22,10 @@ EPS_STD = 1e-5
 ROWS = 512
 NCH = B * N * N // ROWS
 TGT = ROWS // N
-REP = 8
+REP = 4
 FLOPS = 2 * C * F * (B * N * N + 2 * B * N)
 PRELOAD = 4
-SUMMED = NCH - 1
+SUMMED = NCH - 2
 
 
 def tile_gnnlayer_pa_t_kernel(tc, x, e_enc, W_pre, b_pre, out):
@@ -36,7 +36,7 @@ def tile_gnnlayer_pa_t_kernel(tc, x, e_enc, W_pre, b_pre, out):
         ppool = ctx.enter_context(tc.tile_pool(name="ppool", bufs=2))
         gpool = ctx.enter_context(tc.tile_pool(name="gpool", bufs=3))
         qpool = ctx.enter_context(tc.tile_pool(name="qpool", bufs=3))
-        spool = ctx.enter_context(tc.tile_pool(name="spool", bufs=3))
+        spool = ctx.enter_context(tc.tile_pool(name="spool", bufs=2))
         tree = ctx.enter_context(tc.tile_pool(name="tree", bufs=2))
         fpool = ctx.enter_context(tc.tile_pool(name="fpool", bufs=2))
         tpsum = ctx.enter_context(tc.psum_pool(name="tpsum", bufs=4))
@@ -76,6 +76,8 @@ def tile_gnnlayer_pa_t_kernel(tc, x, e_enc, W_pre, b_pre, out):
         accs = {}
         planes = {}
         halves = {}
+        levels = {}
+        token = const.tile([P, 1], U32, name="token")
         fin = {}
 
         def load(c, pieces=1):
@@ -154,6 +156,15 @@ def tile_gnnlayer_pa_t_kernel(tc, x, e_enc, W_pre, b_pre, out):
                 in_=x_s[:, t, :, lo : lo + N].bitcast(I32).unsqueeze(2).to_broadcast([P, 2, REP, N // 4]),
             )
 
+        def send_sources(b):
+            t, lo = divmod(b * N, P)
+            for g in range(2):
+                for dst, src, width in ((xr_q, x_q, N), (xr_s, x_s, N // 4)):
+                    nc.sync.dma_start(
+                        out=dst[:, b, g].bitcast(I32).rearrange("p (d j) -> p d j", d=REP),
+                        in_=src[:, t, g, lo : lo + N].bitcast(I32).unsqueeze(1).to_broadcast([P, REP, width]),
+                    )
+
         def permute(c):
             perm = ppool.tile([P, 4, P], F32, name="perm", tag="perm")
             nc.scalar.copy(
@@ -231,8 +242,8 @@ def tile_gnnlayer_pa_t_kernel(tc, x, e_enc, W_pre, b_pre, out):
         def reduces(c, ft):
             extremes(c, ft, ALU.max, maxs)
             extremes(c, ft, ALU.min, mins)
-            if ft == 0:
-                sums(c, 0)
+            if ft == 0 or c >= SUMMED:
+                sums(c, ft)
 
         def first_level(c):
             if c % 2 == 0:
@@ -242,15 +253,20 @@ def tile_gnnlayer_pa_t_kernel(tc, x, e_enc, W_pre, b_pre, out):
                 out=halves[c // 2][:, :, c % 2, :, :], in0=src[:, :, :, 0 : N // 2], in1=src[:, :, :, N // 2 : N], op=ALU.add
             )
 
-        def upper_levels(c, count):
+        def upper_levels(c, count, widths):
             cols = slice((c + 1 - count) * TGT, (c + 1) * TGT)
             rows = count * TGT
-            cur = halves[c // 2][:, :, 0:count].rearrange("p f c i j -> p f (c i) j")
-            for width in (8, 4, 2):
-                nxt = tree.tile([P, 2, rows, width], F32, name="lvl%d_%d" % (width, count), tag="lvl%d_%d" % (width, count))
-                nc.gpsimd.tensor_tensor(out=nxt[:], in0=cur[:, :, :, 0:width], in1=cur[:, :, :, width : 2 * width], op=ALU.add)
-                cur = nxt[:]
-            nc.gpsimd.tensor_tensor(out=s12[:, :, cols], in0=cur[:, :, :, 0], in1=cur[:, :, :, 1], op=ALU.add)
+            if 8 in widths:
+                levels[c] = halves[c // 2][:, :, 0:count].rearrange("p f c i j -> p f (c i) j")
+            cur = levels[c]
+            for width in widths:
+                if width == 1:
+                    dst = s12[:, :, cols].unsqueeze(3)
+                else:
+                    dst = tree.tile([P, 2, rows, width], F32, name="lvl%d_%d" % (width, count), tag="lvl%d_%d" % (width, count))[:]
+                nc.gpsimd.tensor_tensor(out=dst, in0=cur[:, :, :, 0:width], in1=cur[:, :, :, width : 2 * width], op=ALU.add)
+                cur = dst
+            levels[c] = cur
 
         def target_term():
             tg = tpsum.tile([P, 2, F], F32, name="tg", tag="tp")
@@ -338,8 +354,8 @@ def tile_gnnlayer_pa_t_kernel(tc, x, e_enc, W_pre, b_pre, out):
         load_w(2)
         load(0, 4)
         nc.sync.dma_start(out=x_raw[:, 0, :], in_=x_view[:, 0, :])
-        load(1)
         load_w(1)
+        load(1, 4)
         load(2)
         load(3)
         nc.sync.dma_start(out=x_raw[:, 1, :], in_=x_view[:, 1, :])
@@ -358,14 +374,14 @@ def tile_gnnlayer_pa_t_kernel(tc, x, e_enc, W_pre, b_pre, out):
         regroup_w_vector(5)
         quantise_w(2)
         quantise_chunk(0)
-        front(1)
-        quantise_x(0)
-        regroup_w_vector(2)
+        regroup_w_scalar(2)
         regroup_w_vector(3)
-        repeat_sources(0)
+        quantise_x(0)
         quantise_w(1)
+        repeat_sources(0)
+        front(1)
 
-        LAST = P - TGT
+        LAST = P - 2 * TGT
         for n in range(0, NCH + 1):
             if n + PRELOAD < NCH:
                 load(n + PRELOAD)
@@ -385,11 +401,13 @@ def tile_gnnlayer_pa_t_kernel(tc, x, e_enc, W_pre, b_pre, out):
                 regroup_w_scalar(0)
             if n == 4:
                 regroup_w_scalar(1)
-            if n == 9:
+            if n == 10:
                 finish_tiles(0)
                 means_of_summed(0, P)
             if 1 <= n < NCH:
                 reduces(n - 1, 1)
+            if n % 2 == 0 and n // 2 + 1 < B:
+                repeat_sources(n // 2 + 1)
             if n + 1 < NCH:
                 quantise_chunk(n + 1)
             if 1 <= n < NCH:
@@ -398,34 +416,34 @@ def tile_gnnlayer_pa_t_kernel(tc, x, e_enc, W_pre, b_pre, out):
                 quantise_x(1)
             if n == 6:
                 quantise_w(0)
-            if n % 2 == 0 and n // 2 + 1 < B:
-                repeat_sources(n // 2 + 1)
-            if n < SUMMED:
-                first_level(n)
-                if n % 2 == 1:
-                    upper_levels(n, 2)
-                if n == SUMMED - 1:
-                    upper_levels(n, 1)
+            if n + 1 < NCH:
+                nc.gpsimd.tensor_copy(out=token[:], in_=codes[n + 1][0][:, 0, 0:1])
+            if 1 <= n <= SUMMED:
+                first_level(n - 1)
+            if n >= 2 and n % 2 == 0 and n - 1 < SUMMED:
+                upper_levels(n - 1, 2, (8,))
+            if n >= 3 and n % 2 == 1 and n - 2 < SUMMED:
+                upper_levels(n - 2, 2, (4, 2, 1))
             if n == 9:
                 target_bias()
             if n == 10:
-                variances_of_summed(0, P)
-            if n == 11:
-                clamp_summed(0, P)
-            if n == 12:
-                finish_std(0)
-                turn_means(0)
                 turn_extremes(0, 2, maxs)
+            if n == 11:
+                variances_of_summed(0, P)
+                add_target(0, 2)
                 turn_extremes(0, 1, mins)
+                turn_means(0)
+            if n == 12:
+                clamp_summed(0, P)
+                add_target(0, 0)
+                add_target(0, 1)
             if n == 13:
-                for slot in (0, 2, 1):
-                    add_target(0, slot)
+                finish_std(0)
                 store(0, slice(0, 4))
-            if n == NCH - 1:
-                finish_tiles(1)
-                means_of_summed(1, LAST)
-                variances_of_summed(1, LAST)
         c = NCH - 1
+        finish_tiles(1)
+        means_of_summed(1, LAST)
+        variances_of_summed(1, LAST)
         extremes(c, 1, ALU.max, maxs)
         sums(c, 1)
         extremes(c, 1, ALU.min, mins)

@@ -173,12 +173,13 @@ def tile_gnnlayer_pa_t_kernel(tc, x, e_enc, W_pre, b_pre, out):
             )
             perms[c] = perm
 
-        def front(c):
-            grp = gpool.tile([P, 2, ROWS, 2], F32, name="grp", tag="grp", align_bytes=64)
-            for t in range(4):
+        def front(c, tiles=range(4)):
+            if c not in grps:
+                grps[c] = gpool.tile([P, 2, ROWS, 2], F32, name="grp", tag="grp", align_bytes=64)
+            grp = grps[c]
+            for t in tiles:
                 tp = transpose_permuted(perms[c]) if t == 3 and c in perms else transpose_rows(ets[c][:, t, :])
                 evacuate(tp, grp[:, :, t * P : (t + 1) * P, :])
-            grps[c] = grp
 
         def quantise_chunk(c):
             eq = qpool.tile([P, 2, ROWS], U32, name="eq", tag="eq", align_bytes=64)
@@ -201,20 +202,17 @@ def tile_gnnlayer_pa_t_kernel(tc, x, e_enc, W_pre, b_pre, out):
                 stop=stop,
             )
 
-        def messages(c):
+        def messages(c, ft):
             b = c // 2
             eq, es = codes[c]
-            pair = {}
-            for ft in (1, 0):
-                cols = slice(ft * P, (ft + 1) * P)
-                acc = apsum.tile([P, ROWS], F32, name="acc", tag="acc")
-                mx(acc[:], 4, cols, eq[:, 0, :], es[:, 0, :], True, False)
-                for g in range(2):
-                    for lo in range(0, ROWS, REP * N):
-                        mx(acc[:, lo : lo + REP * N], 2 + g, cols, xr_q[:, b, g, :], xr_s[:, b, g, :], False, False)
-                mx(acc[:], 5, cols, eq[:, 1, :], es[:, 1, :], False, True)
-                pair[ft] = acc
-            accs[c] = pair
+            cols = slice(ft * P, (ft + 1) * P)
+            acc = apsum.tile([P, ROWS], F32, name="acc", tag="acc")
+            mx(acc[:], 4, cols, eq[:, 0, :], es[:, 0, :], True, False)
+            for g in range(2):
+                for lo in range(0, ROWS, REP * N):
+                    mx(acc[:, lo : lo + REP * N], 2 + g, cols, xr_q[:, b, g, :], xr_s[:, b, g, :], False, False)
+            mx(acc[:], 5, cols, eq[:, 1, :], es[:, 1, :], False, True)
+            accs.setdefault(c, {})[ft] = acc
 
         def copies(c):
             if c % 2 == 0:
@@ -388,15 +386,19 @@ def tile_gnnlayer_pa_t_kernel(tc, x, e_enc, W_pre, b_pre, out):
             if n + 2 < NCH:
                 permute(n + 2)
             if n < NCH:
-                messages(n)
-            if n == 8:
-                target_term()
+                messages(n, 1)
+            if n + 2 < NCH:
+                front(n + 2, (0, 1))
             if n < SUMMED:
                 copies(n)
+            if n < NCH:
+                messages(n, 0)
+            if n == 8:
+                target_term()
             if n == 4:
                 front_x(1)
             if n + 2 < NCH:
-                front(n + 2)
+                front(n + 2, (2, 3))
             if n == 3:
                 regroup_w_scalar(0)
             if n == 4:

@@ -25,7 +25,10 @@ TGT = ROWS // N
 REP = 4
 FLOPS = 2 * C * F * (B * N * N + 2 * B * N)
 PRELOAD = 4
+FIRST = 2
 SUMMED = NCH - 2
+BOTH = (13,)
+MOST = 3
 
 
 def tile_gnnlayer_pa_t_kernel(tc, x, e_enc, W_pre, b_pre, out):
@@ -33,7 +36,6 @@ def tile_gnnlayer_pa_t_kernel(tc, x, e_enc, W_pre, b_pre, out):
     with ExitStack() as ctx:
         const = ctx.enter_context(tc.tile_pool(name="const", bufs=1))
         epool = ctx.enter_context(tc.tile_pool(name="epool", bufs=5))
-        ppool = ctx.enter_context(tc.tile_pool(name="ppool", bufs=2))
         gpool = ctx.enter_context(tc.tile_pool(name="gpool", bufs=3))
         qpool = ctx.enter_context(tc.tile_pool(name="qpool", bufs=3))
         spool = ctx.enter_context(tc.tile_pool(name="spool", bufs=2))
@@ -60,7 +62,7 @@ def tile_gnnlayer_pa_t_kernel(tc, x, e_enc, W_pre, b_pre, out):
         c_raw = const.tile([P, 2, F], F32, name="c_raw")
         c_sb = const.tile([P, 2, F], F32, name="c_sb")
         bst = const.tile([P, 2, B * N, 3], F32, name="bst")
-        s12 = const.tile([P, 2, B * N], F32, name="s12")
+        s12 = const.tile([P, 2, 2, B * N], F32, name="s12")
         mins = const.tile([P, 2, B * N], F32, name="mins")
         maxs = const.tile([P, 2, B * N], F32, name="maxs")
 
@@ -70,13 +72,14 @@ def tile_gnnlayer_pa_t_kernel(tc, x, e_enc, W_pre, b_pre, out):
         out_rows = out.flatten_outer_dims()
 
         ets = {}
-        perms = {}
         grps = {}
         codes = {}
         accs = {}
         planes = {}
         halves = {}
         levels = {}
+        tree_units = [(c, ft) for c in range(FIRST, SUMMED) for ft in (1, 0) if ft == 1 or c in BOTH]
+        units = [[(c, ft) for c, ft in ((a, 1), (a + 1, 1), (a, 0), (a + 1, 0)) if (c, ft) in tree_units] for a in range(0, NCH, 2)]
         token = const.tile([P, 1], U32, name="token")
         fin = {}
 
@@ -99,12 +102,6 @@ def tile_gnnlayer_pa_t_kernel(tc, x, e_enc, W_pre, b_pre, out):
             for a in range(4):
                 g, u = divmod(a, 2)
                 nc.tensor.transpose(tp[:, a, :], words[:, 2 * g * P + u : 2 * (g + 1) * P : 2], ident[:])
-            return tp
-
-        def transpose_permuted(perm):
-            tp = tpsum.tile([P, 4, P], F32, name="tp", tag="tp")
-            for a in range(4):
-                nc.tensor.transpose(tp[:, a, :], perm[:, a, :], ident[:])
             return tp
 
         def evacuate(tp, dst):
@@ -165,20 +162,12 @@ def tile_gnnlayer_pa_t_kernel(tc, x, e_enc, W_pre, b_pre, out):
                         in_=src[:, t, g, lo : lo + N].bitcast(I32).unsqueeze(1).to_broadcast([P, REP, width]),
                     )
 
-        def permute(c):
-            perm = ppool.tile([P, 4, P], F32, name="perm", tag="perm")
-            nc.scalar.copy(
-                out=perm[:].rearrange("p (g u) w -> p g u w", u=2),
-                in_=ets[c][:, 3, :].bitcast(F32).rearrange("p (g w u) -> p g u w", g=2, u=2),
-            )
-            perms[c] = perm
-
         def front(c, tiles=range(4)):
             if c not in grps:
                 grps[c] = gpool.tile([P, 2, ROWS, 2], F32, name="grp", tag="grp", align_bytes=64)
             grp = grps[c]
             for t in tiles:
-                tp = transpose_permuted(perms[c]) if t == 3 and c in perms else transpose_rows(ets[c][:, t, :])
+                tp = transpose_rows(ets[c][:, t, :])
                 evacuate(tp, grp[:, :, t * P : (t + 1) * P, :])
 
         def quantise_chunk(c):
@@ -214,12 +203,13 @@ def tile_gnnlayer_pa_t_kernel(tc, x, e_enc, W_pre, b_pre, out):
             mx(acc[:], 5, cols, eq[:, 1, :], es[:, 1, :], False, True)
             accs.setdefault(c, {})[ft] = acc
 
-        def copies(c):
-            if c % 2 == 0:
-                planes[c // 2] = spool.tile([P, 2, 2, ROWS], F32, name="pl", tag="pl")
-            pl = planes[c // 2]
-            nc.scalar.copy(out=pl[:, 0, c % 2, :], in_=accs[c][1][:])
-            nc.scalar.activation(out=pl[:, 1, c % 2, :], in_=accs[c][1][:], func=ACT.Square)
+        def copies(c, ft):
+            pair = c // 2
+            if pair not in planes:
+                planes[pair] = spool.tile([P, 2, MOST, ROWS], F32, name="pl", tag="pl")
+            u = units[pair].index((c, ft))
+            nc.scalar.copy(out=planes[pair][:, 0, u, :], in_=accs[c][ft][:])
+            nc.scalar.activation(out=planes[pair][:, 1, u, :], in_=accs[c][ft][:], func=ACT.Square)
 
         def extremes(c, ft, op, dst):
             nc.vector.tensor_reduce(
@@ -240,31 +230,42 @@ def tile_gnnlayer_pa_t_kernel(tc, x, e_enc, W_pre, b_pre, out):
         def reduces(c, ft):
             extremes(c, ft, ALU.max, maxs)
             extremes(c, ft, ALU.min, mins)
-            if ft == 0 or c >= SUMMED:
+            if (c, ft) not in tree_units:
                 sums(c, ft)
 
-        def first_level(c):
-            if c % 2 == 0:
-                halves[c // 2] = tree.tile([P, 2, 2, TGT, N // 2], F32, name="lvl16", tag="lvl16")
-            src = planes[c // 2][:, :, c % 2, :].rearrange("p f (i j) -> p f i j", j=N)
+        def first_level(c, ft):
+            pair = c // 2
+            count = len(units[pair])
+            if pair not in halves:
+                halves[pair] = tree.tile([P, 2, MOST, TGT, N // 2], F32, name="lvl16", tag="lvl16")
+            u = units[pair].index((c, ft))
+            src = planes[pair][:, :, u, :].rearrange("p f (i j) -> p f i j", j=N)
             nc.gpsimd.tensor_tensor(
-                out=halves[c // 2][:, :, c % 2, :, :], in0=src[:, :, :, 0 : N // 2], in1=src[:, :, :, N // 2 : N], op=ALU.add
+                out=halves[pair][:, :, u, :, :], in0=src[:, :, :, 0 : N // 2], in1=src[:, :, :, N // 2 : N], op=ALU.add
             )
 
-        def upper_levels(c, count, widths):
-            cols = slice((c + 1 - count) * TGT, (c + 1) * TGT)
-            rows = count * TGT
+        def upper_levels(pair, widths):
+            count = len(units[pair])
             if 8 in widths:
-                levels[c] = halves[c // 2][:, :, 0:count].rearrange("p f c i j -> p f (c i) j")
-            cur = levels[c]
+                levels[pair] = halves[pair][:, :, 0:count].rearrange("p f c i j -> p f (c i) j")
+            cur = levels[pair]
             for width in widths:
                 if width == 1:
-                    dst = s12[:, :, cols].unsqueeze(3)
+                    for lo, hi in ((0, 2), (2, count)):
+                        if hi > lo:
+                            c, ft = units[pair][lo]
+                            nc.gpsimd.tensor_tensor(
+                                out=s12[:, :, ft, c * TGT : (c + hi - lo) * TGT].unsqueeze(3),
+                                in0=cur[:, :, lo * TGT : hi * TGT, 0:1],
+                                in1=cur[:, :, lo * TGT : hi * TGT, 1:2],
+                                op=ALU.add,
+                            )
                 else:
-                    dst = tree.tile([P, 2, rows, width], F32, name="lvl%d_%d" % (width, count), tag="lvl%d_%d" % (width, count))[:]
-                nc.gpsimd.tensor_tensor(out=dst, in0=cur[:, :, :, 0:width], in1=cur[:, :, :, width : 2 * width], op=ALU.add)
-                cur = dst
-            levels[c] = cur
+                    tag = "lvl%d" % width
+                    nxt = tree.tile([P, 2, MOST * TGT, width], F32, name=tag, tag=tag)[:, :, 0 : count * TGT, :]
+                    nc.gpsimd.tensor_tensor(out=nxt, in0=cur[:, :, :, 0:width], in1=cur[:, :, :, width : 2 * width], op=ALU.add)
+                    cur = nxt
+            levels[pair] = cur
 
         def target_term():
             tg = tpsum.tile([P, 2, F], F32, name="tg", tag="tp")
@@ -288,40 +289,58 @@ def tile_gnnlayer_pa_t_kernel(tc, x, e_enc, W_pre, b_pre, out):
 
         def finish_tiles(hb):
             fin[hb] = {
-                "mean": fpool.tile([P, P], F32, name="mean", tag="mean"),
+                "mean": fpool.tile([P, 2, P], F32, name="mean", tag="mean"),
                 "var": fpool.tile([P, 2, P], F32, name="var", tag="var"),
-                "msq": fpool.tile([P, P], F32, name="msq", tag="msq"),
+                "msq": fpool.tile([P, 2, P], F32, name="msq", tag="msq"),
                 "res": fpool.tile([P, 4, F], F32, name="res", tag="res"),
             }
 
+        def spans(hb, width, ft, tree_made):
+            runs = []
+            for lo in range(0, width, TGT):
+                if (((hb * P + lo) // TGT, ft) in tree_units) != tree_made:
+                    continue
+                if runs and runs[-1][1] == lo:
+                    runs[-1] = (runs[-1][0], lo + TGT)
+                else:
+                    runs.append((lo, lo + TGT))
+            return [(slice(lo, hi), slice(hb * P + lo, hb * P + hi)) for lo, hi in runs]
+
         def means_of_summed(hb, width):
-            cols = slice(hb * P, hb * P + width)
-            nc.scalar.mul(out=fin[hb]["mean"][:, 0:width], in_=s12[:, 0, cols], mul=1.0 / N)
-            nc.scalar.activation(out=fin[hb]["msq"][:, 0:width], in_=s12[:, 0, cols], func=ACT.Square, scale=1.0 / N)
+            f = fin[hb]
+            for ft in range(2):
+                for cols, src in spans(hb, width, ft, True):
+                    nc.scalar.mul(out=f["mean"][:, ft, cols], in_=s12[:, 0, ft, src], mul=1.0 / N)
+                    nc.scalar.activation(out=f["msq"][:, ft, cols], in_=s12[:, 0, ft, src], func=ACT.Square, scale=1.0 / N)
+                for cols, src in spans(hb, width, ft, False):
+                    nc.scalar.copy(out=f["mean"][:, ft, cols], in_=bst[:, ft, src, 1])
 
         def variances_of_summed(hb, width):
-            cols = slice(hb * P, hb * P + width)
-            nc.vector.tensor_scalar(
-                out=fin[hb]["var"][:, 0, 0:width], in0=bst[:, 0, cols, 2], scalar1=1.0 / N, scalar2=0.0, op0=ALU.mult, op1=ALU.max
-            )
-            nc.vector.scalar_tensor_tensor(
-                out=fin[hb]["var"][:, 1, 0:width],
-                in0=s12[:, 1, cols],
-                scalar=1.0 / N,
-                in1=fin[hb]["msq"][:, 0:width],
-                op0=ALU.mult,
-                op1=ALU.subtract,
-            )
+            f = fin[hb]
+            for ft in range(2):
+                for cols, src in spans(hb, width, ft, True):
+                    nc.vector.scalar_tensor_tensor(
+                        out=f["var"][:, ft, cols],
+                        in0=s12[:, 1, ft, src],
+                        scalar=1.0 / N,
+                        in1=f["msq"][:, ft, cols],
+                        op0=ALU.mult,
+                        op1=ALU.subtract,
+                    )
+                for cols, src in spans(hb, width, ft, False):
+                    nc.vector.tensor_scalar_mul(out=f["var"][:, ft, cols], in0=bst[:, ft, src, 2], scalar1=1.0 / N)
 
         def clamp_summed(hb, width):
-            nc.vector.tensor_scalar_max(out=fin[hb]["var"][:, 1, 0:width], in0=fin[hb]["var"][:, 1, 0:width], scalar1=0.0)
+            nc.vector.tensor_scalar_max(
+                out=fin[hb]["var"][:, :, 0:width], in0=fin[hb]["var"][:, :, 0:width], scalar1=0.0
+            )
 
         def rest(hb, width):
             cols = slice(hb * P + width, (hb + 1) * P)
             nc.vector.tensor_scalar(
                 out=fin[hb]["var"][:, :, width:P], in0=bst[:, :, cols, 2], scalar1=1.0 / N, scalar2=0.0, op0=ALU.mult, op1=ALU.max
             )
-            nc.scalar.copy(out=fin[hb]["mean"][:, width:P], in_=bst[:, 1, cols, 1])
+            nc.scalar.copy(out=fin[hb]["mean"][:, :, width:P], in_=bst[:, :, cols, 1])
 
         def turn(name, planes2):
             tp = tpsum.tile([P, 2, P], F32, name=name, tag="tp")
@@ -341,10 +360,17 @@ def tile_gnnlayer_pa_t_kernel(tc, x, e_enc, W_pre, b_pre, out):
             nc.scalar.activation(out=fin[hb]["res"][:, 3, :], in_=fv, func=ACT.Sqrt, bias=eps_t[:])
 
         def turn_means(hb):
-            fin[hb]["t0"] = turn("fm", [bst[:, 0, hb * P : (hb + 1) * P, 1], fin[hb]["mean"][:]])
+            fin[hb]["t0"] = turn("fm", [fin[hb]["mean"][:, 0, :], fin[hb]["mean"][:, 1, :]])
 
         def turn_extremes(hb, slot, src):
             fin[hb]["t%d" % slot] = turn("fx", [src[:, ft, hb * P : (hb + 1) * P] for ft in range(2)])
+
+        def bring_out(hb, slot):
+            nc.scalar.copy(out=fin[hb]["res"][:, slot, :], in_=fin[hb]["t%d" % slot])
+
+        def add_target_gpsimd(hb, slot):
+            res = fin[hb]["res"][:, slot, :]
+            nc.gpsimd.tensor_tensor(out=res, in0=res, in1=c_sb[:, hb, :], op=ALU.add)
 
         def add_target(hb, slot):
             nc.vector.tensor_tensor(out=fin[hb]["res"][:, slot, :], in0=fin[hb]["t%d" % slot], in1=c_sb[:, hb, :], op=ALU.add)
@@ -383,14 +409,12 @@ def tile_gnnlayer_pa_t_kernel(tc, x, e_enc, W_pre, b_pre, out):
         for n in range(0, NCH + 1):
             if n + PRELOAD < NCH:
                 load(n + PRELOAD)
-            if n + 2 < NCH:
-                permute(n + 2)
             if n < NCH:
                 messages(n, 1)
             if n + 2 < NCH:
                 front(n + 2, (0, 1))
-            if n < SUMMED:
-                copies(n)
+            if FIRST <= n < SUMMED:
+                copies(n, 1)
             if n < NCH:
                 messages(n, 0)
             if n == 8:
@@ -399,6 +423,8 @@ def tile_gnnlayer_pa_t_kernel(tc, x, e_enc, W_pre, b_pre, out):
                 front_x(1)
             if n + 2 < NCH:
                 front(n + 2, (2, 3))
+            if n in BOTH:
+                copies(n, 0)
             if n == 3:
                 regroup_w_scalar(0)
             if n == 4:
@@ -418,49 +444,53 @@ def tile_gnnlayer_pa_t_kernel(tc, x, e_enc, W_pre, b_pre, out):
                 quantise_x(1)
             if n == 6:
                 quantise_w(0)
-            if n + 1 < NCH:
+            if FIRST < n < NCH - 2:
                 nc.gpsimd.tensor_copy(out=token[:], in_=codes[n + 1][0][:, 0, 0:1])
-            if 1 <= n <= SUMMED:
-                first_level(n - 1)
-            if n >= 2 and n % 2 == 0 and n - 1 < SUMMED:
-                upper_levels(n - 1, 2, (8,))
-            if n >= 3 and n % 2 == 1 and n - 2 < SUMMED:
-                upper_levels(n - 2, 2, (4, 2, 1))
+            for ft in (1, 0):
+                if (n - 1, ft) in tree_units:
+                    first_level(n - 1, ft)
+            if n >= FIRST + 2 and n % 2 == 0 and n - 1 < SUMMED:
+                upper_levels((n - 1) // 2, (8,))
+            if n >= FIRST + 3 and n % 2 == 1 and n - 2 < SUMMED:
+                upper_levels((n - 2) // 2, (4, 2, 1))
             if n == 9:
                 target_bias()
             if n == 10:
                 turn_extremes(0, 2, maxs)
+                bring_out(0, 2)
+                turn_extremes(0, 1, mins)
+                bring_out(0, 1)
             if n == 11:
                 variances_of_summed(0, P)
-                add_target(0, 2)
-                turn_extremes(0, 1, mins)
                 turn_means(0)
+                bring_out(0, 0)
+                for slot in (2, 1):
+                    add_target_gpsimd(0, slot)
             if n == 12:
                 clamp_summed(0, P)
-                add_target(0, 0)
-                add_target(0, 1)
+                add_target_gpsimd(0, 0)
             if n == 13:
                 finish_std(0)
                 store(0, slice(0, 4))
         c = NCH - 1
         finish_tiles(1)
-        means_of_summed(1, LAST)
-        variances_of_summed(1, LAST)
         extremes(c, 1, ALU.max, maxs)
         sums(c, 1)
         extremes(c, 1, ALU.min, mins)
-        clamp_summed(1, LAST)
-        sums(c, 0)
         extremes(c, 0, ALU.max, maxs)
-        rest(1, LAST)
-        finish_std(1)
-        turn_means(1)
         turn_extremes(1, 2, maxs)
-        store(1, slice(3, 4))
         extremes(c, 0, ALU.min, mins)
         turn_extremes(1, 1, mins)
-        add_target(1, 0)
+        means_of_summed(1, LAST)
+        sums(c, 0)
+        variances_of_summed(1, LAST)
+        rest(1, LAST)
         add_target(1, 2)
+        clamp_summed(1, LAST)
+        turn_means(1)
+        finish_std(1)
         add_target(1, 1)
-        store(1, slice(2, 3))
-        store(1, slice(0, 2))
+        store(1, slice(1, 3))
+        add_target(1, 0)
+        store(1, slice(0, 1))
+        store(1, slice(3, 4))

@@ -27,6 +27,7 @@ FLOPS = 2 * C * F * (B * N * N + 2 * B * N)
 PRELOAD = 4
 FIRST = 2
 SUMMED = NCH - 2
+TREE = (2, 3, 5, 7, 9, 11, 12, 13)
 BOTH = (13,)
 MOST = 3
 
@@ -78,7 +79,7 @@ def tile_gnnlayer_pa_t_kernel(tc, x, e_enc, W_pre, b_pre, out):
         planes = {}
         halves = {}
         levels = {}
-        tree_units = [(c, ft) for c in range(FIRST, SUMMED) for ft in (1, 0) if ft == 1 or c in BOTH]
+        tree_units = [(c, ft) for c in TREE for ft in (1, 0) if ft == 1 or c in BOTH]
         units = [[(c, ft) for c, ft in ((a, 1), (a + 1, 1), (a, 0), (a + 1, 0)) if (c, ft) in tree_units] for a in range(0, NCH, 2)]
         token = const.tile([P, 1], U32, name="token")
         fin = {}
@@ -251,7 +252,8 @@ def tile_gnnlayer_pa_t_kernel(tc, x, e_enc, W_pre, b_pre, out):
             cur = levels[pair]
             for width in widths:
                 if width == 1:
-                    for lo, hi in ((0, 2), (2, count)):
+                    upper = sum(ft for c, ft in units[pair])
+                    for lo, hi in ((0, upper), (upper, count)):
                         if hi > lo:
                             c, ft = units[pair][lo]
                             nc.gpsimd.tensor_tensor(
@@ -397,9 +399,9 @@ def tile_gnnlayer_pa_t_kernel(tc, x, e_enc, W_pre, b_pre, out):
         regroup_w_vector(4)
         regroup_w_vector(5)
         quantise_w(2)
-        quantise_chunk(0)
         regroup_w_scalar(2)
         regroup_w_vector(3)
+        quantise_chunk(0)
         quantise_x(0)
         quantise_w(1)
         repeat_sources(0)
@@ -413,7 +415,7 @@ def tile_gnnlayer_pa_t_kernel(tc, x, e_enc, W_pre, b_pre, out):
                 messages(n, 1)
             if n + 2 < NCH:
                 front(n + 2, (0, 1))
-            if FIRST <= n < SUMMED:
+            if n in TREE:
                 copies(n, 1)
             if n < NCH:
                 messages(n, 0)
@@ -444,7 +446,7 @@ def tile_gnnlayer_pa_t_kernel(tc, x, e_enc, W_pre, b_pre, out):
                 quantise_x(1)
             if n == 6:
                 quantise_w(0)
-            if FIRST < n < NCH - 2:
+            if n - 1 in TREE and n < NCH - 2:
                 nc.gpsimd.tensor_copy(out=token[:], in_=codes[n + 1][0][:, 0, 0:1])
             for ft in (1, 0):
                 if (n - 1, ft) in tree_units:

@@ -29,6 +29,7 @@ FIRST = 2
 SUMMED = NCH - 2
 TREE = (2, 3, 5, 7, 9, 11, 12, 13)
 BOTH = (13,)
+ALONE = 14
 MOST = 3
 
 
@@ -80,6 +81,8 @@ def tile_gnnlayer_pa_t_kernel(tc, x, e_enc, W_pre, b_pre, out):
         halves = {}
         levels = {}
         tree_units = [(c, ft) for c in TREE for ft in (1, 0) if ft == 1 or c in BOTH]
+        summed_units = tree_units + [(ALONE, 1)]
+        junk = const.tile([P, ROWS], F32, name="junk")
         units = [[(c, ft) for c, ft in ((a, 1), (a + 1, 1), (a, 0), (a + 1, 0)) if (c, ft) in tree_units] for a in range(0, NCH, 2)]
         token = const.tile([P, 1], U32, name="token")
         fin = {}
@@ -192,17 +195,21 @@ def tile_gnnlayer_pa_t_kernel(tc, x, e_enc, W_pre, b_pre, out):
                 stop=stop,
             )
 
+        def open_messages(c, ft):
+            eq, es = codes[c]
+            acc = apsum.tile([P, ROWS], F32, name="acc", tag="acc")
+            mx(acc[:], 4, slice(ft * P, (ft + 1) * P), eq[:, 0, :], es[:, 0, :], True, False)
+            accs.setdefault(c, {})[ft] = acc
+
         def messages(c, ft):
             b = c // 2
             eq, es = codes[c]
             cols = slice(ft * P, (ft + 1) * P)
-            acc = apsum.tile([P, ROWS], F32, name="acc", tag="acc")
-            mx(acc[:], 4, cols, eq[:, 0, :], es[:, 0, :], True, False)
+            acc = accs[c][ft]
             for g in range(2):
                 for lo in range(0, ROWS, REP * N):
                     mx(acc[:, lo : lo + REP * N], 2 + g, cols, xr_q[:, b, g, :], xr_s[:, b, g, :], False, False)
             mx(acc[:], 5, cols, eq[:, 1, :], es[:, 1, :], False, True)
-            accs.setdefault(c, {})[ft] = acc
 
         def copies(c, ft):
             pair = c // 2
@@ -211,6 +218,17 @@ def tile_gnnlayer_pa_t_kernel(tc, x, e_enc, W_pre, b_pre, out):
             u = units[pair].index((c, ft))
             nc.scalar.copy(out=planes[pair][:, 0, u, :], in_=accs[c][ft][:])
             nc.scalar.activation(out=planes[pair][:, 1, u, :], in_=accs[c][ft][:], func=ACT.Square)
+
+        def row_sums(c):
+            pl = spool.tile([P, 2, MOST, ROWS], F32, name="pl", tag="pl")[:, 0, 0, :]
+            nc.scalar.copy(out=pl, in_=accs[c][1][:])
+            for which, func in ((0, ACT.Copy), (1, ACT.Square)):
+                for i in range(TGT):
+                    cols = slice(i * N, (i + 1) * N)
+                    col = c * TGT + i
+                    nc.scalar.activation(
+                        out=junk[:, cols], in_=pl[:, cols], func=func, accum_out=s12[:, which, 1, col : col + 1]
+                    )
 
         def extremes(c, ft, op, dst):
             nc.vector.tensor_reduce(
@@ -231,7 +249,7 @@ def tile_gnnlayer_pa_t_kernel(tc, x, e_enc, W_pre, b_pre, out):
         def reduces(c, ft):
             extremes(c, ft, ALU.max, maxs)
             extremes(c, ft, ALU.min, mins)
-            if (c, ft) not in tree_units:
+            if (c, ft) not in summed_units:
                 sums(c, ft)
 
         def first_level(c, ft):
@@ -300,7 +318,7 @@ def tile_gnnlayer_pa_t_kernel(tc, x, e_enc, W_pre, b_pre, out):
         def spans(hb, width, ft, tree_made):
             runs = []
             for lo in range(0, width, TGT):
-                if (((hb * P + lo) // TGT, ft) in tree_units) != tree_made:
+                if (((hb * P + lo) // TGT, ft) in summed_units) != tree_made:
                     continue
                 if runs and runs[-1][1] == lo:
                     runs[-1] = (runs[-1][0], lo + TGT)
@@ -407,18 +425,25 @@ def tile_gnnlayer_pa_t_kernel(tc, x, e_enc, W_pre, b_pre, out):
         repeat_sources(0)
         front(1)
 
-        LAST = P - 2 * TGT
+        LAST = P - TGT
         for n in range(0, NCH + 1):
             if n + PRELOAD < NCH:
                 load(n + PRELOAD)
             if n < NCH:
+                open_messages(n, 1)
+                if n == 0:
+                    open_messages(n, 0)
                 messages(n, 1)
             if n + 2 < NCH:
                 front(n + 2, (0, 1))
             if n in TREE:
                 copies(n, 1)
             if n < NCH:
+                if n > 0:
+                    open_messages(n, 0)
                 messages(n, 0)
+            if n == ALONE:
+                row_sums(n)
             if n == 8:
                 target_term()
             if n == 4:

from contextlib import ExitStack

import concourse.mybir as mybir
from concourse.masks import make_identity

F32 = mybir.dt.float32
BF16 = mybir.dt.bfloat16
I32 = mybir.dt.int32
U32 = mybir.dt.uint32
U8 = mybir.dt.uint8
FP8X4 = mybir.dt.float8_e4m3fn_x4
ALU = mybir.AluOpType
ACT = mybir.ActivationFunctionType
AX = mybir.AxisListType

P = 128
B = 8
N = 32
C = 1024
F = 256
EPS_STD = 1e-5
ROWS = 512
NCH = B * N * N // ROWS
TGT = ROWS // N
REP = 4
FLOPS = 2 * C * F * (B * N * N + 2 * B * N)
PRELOAD = 4
FIRST = 2
SUMMED = NCH - 2
TREE = (2, 3, 5, 7, 9, 11, 12, 13)
BOTH = (13,)
ALONE = 14
MOST = 3


def tile_gnnlayer_pa_t_kernel(tc, x, e_enc, W_pre, b_pre, out):
    nc = tc.nc
    with ExitStack() as ctx:
        const = ctx.enter_context(tc.tile_pool(name="const", bufs=1))
        epool = ctx.enter_context(tc.tile_pool(name="epool", bufs=5))
        gpool = ctx.enter_context(tc.tile_pool(name="gpool", bufs=3))
        qpool = ctx.enter_context(tc.tile_pool(name="qpool", bufs=3))
        spool = ctx.enter_context(tc.tile_pool(name="spool", bufs=2))
        tree = ctx.enter_context(tc.tile_pool(name="tree", bufs=2))
        fpool = ctx.enter_context(tc.tile_pool(name="fpool", bufs=2))
        tpsum = ctx.enter_context(tc.psum_pool(name="tpsum", bufs=4))
        apsum = ctx.enter_context(tc.psum_pool(name="apsum", bufs=4))
        ctx.enter_context(tc.manual_schedule())

        eps_t = const.tile([P, 1], F32, name="eps_t")
        warm = const.tile([P, 1], F32, name="warm")
        ident = const.tile([P, P], F32, name="ident")
        w_raw = const.tile([P, 6, 4, F], BF16, name="w_raw")
        w_grp = const.tile([P, 6, F, 4], BF16, name="w_grp", align_bytes=64)
        w_q = const.tile([P, 6, F], U32, name="w_q", align_bytes=64)
        w_s = const.tile([P, 6, F], U8, name="w_s", align_bytes=64)
        x_raw = const.tile([P, 2, C], BF16, name="x_raw")
        x_grp = const.tile([P, 2, 2, P, 2], F32, name="x_grp", align_bytes=64)
        x_q = const.tile([P, 2, 2, P], U32, name="x_q", align_bytes=64)
        x_s = const.tile([P, 2, 2, P], U8, name="x_s", align_bytes=64)
        xr_q = const.tile([P, B, 2, REP * N], U32, name="xr_q", align_bytes=64)
        xr_s = const.tile([P, B, 2, REP * N], U8, name="xr_s", align_bytes=64)
        bias_bc = const.tile([P, F], BF16, name="bias_bc")
        c_raw = const.tile([P, 2, F], F32, name="c_raw")
        c_sb = const.tile([P, 2, F], F32, name="c_sb")
        bst = const.tile([P, 2, B * N, 3], F32, name="bst")
        s12 = const.tile([P, 2, 2, B * N], F32, name="s12")
        mins = const.tile([P, 2, B * N], F32, name="mins")
        maxs = const.tile([P, 2, B * N], F32, name="maxs")

        w_view = W_pre.rearrange("(s q t) c -> q s t c", q=P, t=4)
        x_view = x.flatten_outer_dims().rearrange("(t p) k -> p t k", p=P)
        e_view = e_enc.flatten_outer_dims().rearrange("(c t p) k -> c p t k", t=4, p=P)
        out_rows = out.flatten_outer_dims()

        ets = {}
        grps = {}
        codes = {}
        accs = {}
        planes = {}
        halves = {}
        levels = {}
        tree_units = [(c, ft) for c in TREE for ft in (1, 0) if ft == 1 or c in BOTH]
        summed_units = tree_units + [(ALONE, 1)]
        junk = const.tile([P, ROWS], F32, name="junk")
        units = [[(c, ft) for c, ft in ((a, 1), (a + 1, 1), (a, 0), (a + 1, 0)) if (c, ft) in tree_units] for a in range(0, NCH, 2)]
        token = const.tile([P, 1], U32, name="token")
        fin = {}

        def load(c, pieces=1):
            et = epool.tile([P, 4, C], BF16, name="et", tag="et")
            step = 4 // pieces
            for t in range(0, 4, step):
                nc.sync.dma_start(out=et[:, t : t + step, :], in_=e_view[c][:, t : t + step, :])
            ets[c] = et

        def load_w(block):
            nc.sync.dma_start(out=w_raw[:, 2 * block : 2 * block + 2], in_=w_view[:, 2 * block : 2 * block + 2])

        def load_x(t):
            nc.sync.dma_start(out=x_raw[:, t, :], in_=x_view[:, t, :])

        def transpose_rows(rows):
            tp = tpsum.tile([P, 4, P], F32, name="tp", tag="tp")
            words = rows.bitcast(F32)
            for a in range(4):
                g, u = divmod(a, 2)
                nc.tensor.transpose(tp[:, a, :], words[:, 2 * g * P + u : 2 * (g + 1) * P : 2], ident[:])
            return tp

        def evacuate(tp, dst):
            nc.scalar.copy(out=dst, in_=tp[:].rearrange("p (g u) r -> p g r u", u=2))

        def quantise(src, q_ap, s_ap):
            nc.vector.quantize_mx(out=q_ap.bitcast(FP8X4), scales=s_ap, in_=src)

        def quantise_w(block):
            lo = 2 * block
            quantise(
                w_grp[:, lo : lo + 2].rearrange("p s c t -> p (s c t)"),
                w_q[:, lo : lo + 2].rearrange("p s c -> p (s c)"),
                w_s[:, lo : lo + 2].rearrange("p s c -> p (s c)"),
            )

        def regroup_views(s):
            return (
                w_grp[:, s].rearrange("p (c i) t -> p c t i", i=4),
                w_raw[:, s].rearrange("p t (c i) -> p c t i", i=4),
            )

        def regroup_w_vector(s):
            dst, src = regroup_views(s)
            nc.vector.tensor_copy(out=dst, in_=src)

        def regroup_w_scalar(s):
            dst, src = regroup_views(s)
            nc.scalar.copy(out=dst, in_=src)

        def front_x(t):
            evacuate(transpose_rows(x_raw[:, t, :]), x_grp[:, t])

        def quantise_x(t):
            quantise(
                x_grp[:, t].rearrange("p g n u -> p (g n u)").bitcast(BF16),
                x_q[:, t].rearrange("p g n -> p (g n)"),
                x_s[:, t].rearrange("p g n -> p (g n)"),
            )

        def repeat_sources(b):
            t, lo = divmod(b * N, P)
            nc.vector.tensor_copy(
                out=xr_q[:, b].bitcast(I32).rearrange("p g (d j) -> p g d j", d=REP),
                in_=x_q[:, t, :, lo : lo + N].bitcast(I32).unsqueeze(2).to_broadcast([P, 2, REP, N]),
            )
            nc.vector.tensor_copy(
                out=xr_s[:, b].bitcast(I32).rearrange("p g (d j) -> p g d j", d=REP),
                in_=x_s[:, t, :, lo : lo + N].bitcast(I32).unsqueeze(2).to_broadcast([P, 2, REP, N // 4]),
            )

        def send_sources(b):
            t, lo = divmod(b * N, P)
            for g in range(2):
                for dst, src, width in ((xr_q, x_q, N), (xr_s, x_s, N // 4)):
                    nc.sync.dma_start(
                        out=dst[:, b, g].bitcast(I32).rearrange("p (d j) -> p d j", d=REP),
                        in_=src[:, t, g, lo : lo + N].bitcast(I32).unsqueeze(1).to_broadcast([P, REP, width]),
                    )

        def front(c, tiles=range(4)):
            if c not in grps:
                grps[c] = gpool.tile([P, 2, ROWS, 2], F32, name="grp", tag="grp", align_bytes=64)
            grp = grps[c]
            for t in tiles:
                tp = transpose_rows(ets[c][:, t, :])
                evacuate(tp, grp[:, :, t * P : (t + 1) * P, :])

        def quantise_chunk(c):
            eq = qpool.tile([P, 2, ROWS], U32, name="eq", tag="eq", align_bytes=64)
            es = qpool.tile([P, 2, ROWS], U8, name="es", tag="es", align_bytes=64)
            quantise(
                grps[c][:].rearrange("p g n u -> p (g n u)").bitcast(BF16),
                eq[:].rearrange("p g n -> p (g n)"),
                es[:].rearrange("p g n -> p (g n)"),
            )
            codes[c] = (eq, es)

        def mx(out_ap, s, cols, rhs, rhs_scale, start, stop):
            nc.tensor.matmul_mx(
                out=out_ap,
                lhsT=w_q[:, s, cols].bitcast(FP8X4),
                lhsT_scale=w_s[:, s, cols],
                rhs=rhs.bitcast(FP8X4),
                rhs_scale=rhs_scale,
                start=start,
                stop=stop,
            )

        def open_messages(c, ft):
            eq, es = codes[c]
            acc = apsum.tile([P, ROWS], F32, name="acc", tag="acc")
            mx(acc[:], 4, slice(ft * P, (ft + 1) * P), eq[:, 0, :], es[:, 0, :], True, False)
            accs.setdefault(c, {})[ft] = acc

        def messages(c, ft):
            b = c // 2
            eq, es = codes[c]
            cols = slice(ft * P, (ft + 1) * P)
            acc = accs[c][ft]
            for g in range(2):
                for lo in range(0, ROWS, REP * N):
                    mx(acc[:, lo : lo + REP * N], 2 + g, cols, xr_q[:, b, g, :], xr_s[:, b, g, :], False, False)
            mx(acc[:], 5, cols, eq[:, 1, :], es[:, 1, :], False, True)

        def copies(c, ft):
            pair = c // 2
            if pair not in planes:
                planes[pair] = spool.tile([P, 2, MOST, ROWS], F32, name="pl", tag="pl")
            u = units[pair].index((c, ft))
            nc.scalar.copy(out=planes[pair][:, 0, u, :], in_=accs[c][ft][:])
            nc.scalar.activation(out=planes[pair][:, 1, u, :], in_=accs[c][ft][:], func=ACT.Square)

        def row_sums(c):
            pl = spool.tile([P, 2, MOST, ROWS], F32, name="pl", tag="pl")[:, 0, 0, :]
            nc.scalar.copy(out=pl, in_=accs[c][1][:])
            for which, func in ((0, ACT.Copy), (1, ACT.Square)):
                for i in range(TGT):
                    cols = slice(i * N, (i + 1) * N)
                    col = c * TGT + i
                    nc.scalar.activation(
                        out=junk[:, cols], in_=pl[:, cols], func=func, accum_out=s12[:, which, 1, col : col + 1]
                    )

        def extremes(c, ft, op, dst):
            nc.vector.tensor_reduce(
                out=dst[:, ft, c * TGT : (c + 1) * TGT],
                in_=accs[c][ft][:].rearrange("p (i j) -> p i j", j=N),
                axis=AX.X,
                op=op,
            )

        def sums(c, ft):
            m = accs[c][ft][:].rearrange("p (i j) -> p i j", j=N)
            for i in range(0, TGT, 2):
                nc.vector.bn_stats(
                    out=bst[:, ft, c * TGT + i : c * TGT + i + 2, :].rearrange("p m s -> p (m s)"),
                    in_=m[:, i : i + 2, :].rearrange("p m j -> p j m"),
                )

        def reduces(c, ft):
            extremes(c, ft, ALU.max, maxs)
            extremes(c, ft, ALU.min, mins)
            if (c, ft) not in summed_units:
                sums(c, ft)

        def first_level(c, ft):
            pair = c // 2
            count = len(units[pair])
            if pair not in halves:
                halves[pair] = tree.tile([P, 2, MOST, TGT, N // 2], F32, name="lvl16", tag="lvl16")
            u = units[pair].index((c, ft))
            src = planes[pair][:, :, u, :].rearrange("p f (i j) -> p f i j", j=N)
            nc.gpsimd.tensor_tensor(
                out=halves[pair][:, :, u, :, :], in0=src[:, :, :, 0 : N // 2], in1=src[:, :, :, N // 2 : N], op=ALU.add
            )

        def upper_levels(pair, widths):
            count = len(units[pair])
            if 8 in widths:
                levels[pair] = halves[pair][:, :, 0:count].rearrange("p f c i j -> p f (c i) j")
            cur = levels[pair]
            for width in widths:
                if width == 1:
                    upper = sum(ft for c, ft in units[pair])
                    for lo, hi in ((0, upper), (upper, count)):
                        if hi > lo:
                            c, ft = units[pair][lo]
                            nc.gpsimd.tensor_tensor(
                                out=s12[:, :, ft, c * TGT : (c + hi - lo) * TGT].unsqueeze(3),
                                in0=cur[:, :, lo * TGT : hi * TGT, 0:1],
                                in1=cur[:, :, lo * TGT : hi * TGT, 1:2],
                                op=ALU.add,
                            )
                else:
                    tag = "lvl%d" % width
                    nxt = tree.tile([P, 2, MOST * TGT, width], F32, name=tag, tag=tag)[:, :, 0 : count * TGT, :]
                    nc.gpsimd.tensor_tensor(out=nxt, in0=cur[:, :, :, 0:width], in1=cur[:, :, :, width : 2 * width], op=ALU.add)
                    cur = nxt
            levels[pair] = cur

        def target_term():
            tg = tpsum.tile([P, 2, F], F32, name="tg", tag="tp")
            for hb in range(2):
                for g in range(2):
                    nc.tensor.matmul_mx(
                        out=tg[:, hb, :],
                        lhsT=x_q[:, hb, g, :].bitcast(FP8X4),
                        lhsT_scale=x_s[:, hb, g, :],
                        rhs=w_q[:, g, :].bitcast(FP8X4),
                        rhs_scale=w_s[:, g, :],
                        start=(g == 0),
                        stop=(g == 1),
                    )
            nc.scalar.copy(out=c_raw[:], in_=tg[:])

        def target_bias():
            nc.gpsimd.tensor_tensor(
                out=c_sb[:], in0=c_raw[:], in1=bias_bc[:].unsqueeze(1).to_broadcast([P, 2, F]), op=ALU.add
            )

        def finish_tiles(hb):
            fin[hb] = {
                "mean": fpool.tile([P, 2, P], F32, name="mean", tag="mean"),
                "var": fpool.tile([P, 2, P], F32, name="var", tag="var"),
                "msq": fpool.tile([P, 2, P], F32, name="msq", tag="msq"),
                "res": fpool.tile([P, 4, F], F32, name="res", tag="res"),
            }

        def spans(hb, width, ft, tree_made):
            runs = []
            for lo in range(0, width, TGT):
                if (((hb * P + lo) // TGT, ft) in summed_units) != tree_made:
                    continue
                if runs and runs[-1][1] == lo:
                    runs[-1] = (runs[-1][0], lo + TGT)
                else:
                    runs.append((lo, lo + TGT))
            return [(slice(lo, hi), slice(hb * P + lo, hb * P + hi)) for lo, hi in runs]

        def means_of_summed(hb, width):
            f = fin[hb]
            for ft in range(2):
                for cols, src in spans(hb, width, ft, True):
                    nc.scalar.mul(out=f["mean"][:, ft, cols], in_=s12[:, 0, ft, src], mul=1.0 / N)
                    nc.scalar.activation(out=f["msq"][:, ft, cols], in_=s12[:, 0, ft, src], func=ACT.Square, scale=1.0 / N)
                for cols, src in spans(hb, width, ft, False):
                    nc.scalar.copy(out=f["mean"][:, ft, cols], in_=bst[:, ft, src, 1])

        def variances_of_summed(hb, width):
            f = fin[hb]
            for ft in range(2):
                for cols, src in spans(hb, width, ft, True):
                    nc.vector.scalar_tensor_tensor(
                        out=f["var"][:, ft, cols],
                        in0=s12[:, 1, ft, src],
                        scalar=1.0 / N,
                        in1=f["msq"][:, ft, cols],
                        op0=ALU.mult,
                        op1=ALU.subtract,
                    )
                for cols, src in spans(hb, width, ft, False):
                    nc.vector.tensor_scalar_mul(out=f["var"][:, ft, cols], in0=bst[:, ft, src, 2], scalar1=1.0 / N)

        def clamp_summed(hb, width):
            nc.vector.tensor_scalar_max(
                out=fin[hb]["var"][:, :, 0:width], in0=fin[hb]["var"][:, :, 0:width], scalar1=0.0
            )

        def rest(hb, width):
            cols = slice(hb * P + width, (hb + 1) * P)
            nc.vector.tensor_scalar(
                out=fin[hb]["var"][:, :, width:P], in0=bst[:, :, cols, 2], scalar1=1.0 / N, scalar2=0.0, op0=ALU.mult, op1=ALU.max
            )
            nc.scalar.copy(out=fin[hb]["mean"][:, :, width:P], in_=bst[:, :, cols, 1])

        def turn(name, planes2):
            tp = tpsum.tile([P, 2, P], F32, name=name, tag="tp")
            for ft in range(2):
                nc.tensor.transpose(tp[:, ft, :], planes2[ft], ident[:])
            return tp[:].rearrange("p f r -> p (f r)")

        def store(hb, slots):
            rows = slice(hb * P, (hb + 1) * P)
            nc.sync.dma_start(
                out=out_rows[rows, slots.start * F : slots.stop * F],
                in_=fin[hb]["res"][:, slots].rearrange("p s f -> p (s f)"),
            )

        def finish_std(hb):
            fv = turn("fv", [fin[hb]["var"][:, 0, :], fin[hb]["var"][:, 1, :]])
            nc.scalar.activation(out=fin[hb]["res"][:, 3, :], in_=fv, func=ACT.Sqrt, bias=eps_t[:])

        def turn_means(hb):
            fin[hb]["t0"] = turn("fm", [fin[hb]["mean"][:, 0, :], fin[hb]["mean"][:, 1, :]])

        def turn_extremes(hb, slot, src):
            fin[hb]["t%d" % slot] = turn("fx", [src[:, ft, hb * P : (hb + 1) * P] for ft in range(2)])

        def bring_out(hb, slot):
            nc.scalar.copy(out=fin[hb]["res"][:, slot, :], in_=fin[hb]["t%d" % slot])

        def add_target_gpsimd(hb, slot):
            res = fin[hb]["res"][:, slot, :]
            nc.gpsimd.tensor_tensor(out=res, in0=res, in1=c_sb[:, hb, :], op=ALU.add)

        def add_target(hb, slot):
            nc.vector.tensor_tensor(out=fin[hb]["res"][:, slot, :], in0=fin[hb]["t%d" % slot], in1=c_sb[:, hb, :], op=ALU.add)

        load_w(2)
        load(0, 4)
        nc.sync.dma_start(out=x_raw[:, 0, :], in_=x_view[:, 0, :])
        load_w(1)
        load(1, 4)
        load(2)
        load(3)
        nc.sync.dma_start(out=x_raw[:, 1, :], in_=x_view[:, 1, :])
        load_w(0)
        nc.sync.dma_start(out=bias_bc[:], in_=b_pre.partition_broadcast(P))

        nc.vector.memset(eps_t[:], EPS_STD)
        nc.vector.memset(warm[:], 1.0)
        nc.vector.memset(x_s[:].rearrange("p t g n -> p (t g n)").bitcast(I32), 0)
        nc.scalar.sqrt(warm[:], warm[:])
        make_identity(nc, ident[:])

        front(0)
        front_x(0)
        regroup_w_vector(4)
        regroup_w_vector(5)
        quantise_w(2)
        regroup_w_scalar(2)
        regroup_w_vector(3)
        quantise_chunk(0)
        quantise_x(0)
        quantise_w(1)
        repeat_sources(0)
        front(1)

        LAST = P - TGT
        for n in range(0, NCH + 1):
            if n + PRELOAD < NCH:
                load(n + PRELOAD)
            if n < NCH:
                open_messages(n, 1)
                if n == 0:
                    open_messages(n, 0)
                messages(n, 1)
            if n + 2 < NCH:
                front(n + 2, (0, 1))
            if n in TREE:
                copies(n, 1)
            if n < NCH:
                if n > 0:
                    open_messages(n, 0)
                messages(n, 0)
            if n == ALONE:
                row_sums(n)
            if n == 8:
                target_term()
            if n == 4:
                front_x(1)
            if n + 2 < NCH:
                front(n + 2, (2, 3))
            if n in BOTH:
                copies(n, 0)
            if n == 3:
                regroup_w_scalar(0)
            if n == 4:
                regroup_w_scalar(1)
            if n == 10:
                finish_tiles(0)
                means_of_summed(0, P)
            if 1 <= n < NCH:
                reduces(n - 1, 1)
            if n % 2 == 0 and n // 2 + 1 < B:
                repeat_sources(n // 2 + 1)
            if n + 1 < NCH:
                quantise_chunk(n + 1)
            if 1 <= n < NCH:
                reduces(n - 1, 0)
            if n == 5:
                quantise_x(1)
            if n == 6:
                quantise_w(0)
            if n - 1 in TREE and n < NCH - 2:
                nc.gpsimd.tensor_copy(out=token[:], in_=codes[n + 1][0][:, 0, 0:1])
            for ft in (1, 0):
                if (n - 1, ft) in tree_units:
                    first_level(n - 1, ft)
            if n >= FIRST + 2 and n % 2 == 0 and n - 1 < SUMMED:
                upper_levels((n - 1) // 2, (8,))
            if n >= FIRST + 3 and n % 2 == 1 and n - 2 < SUMMED:
                upper_levels((n - 2) // 2, (4, 2, 1))
            if n == 9:
                target_bias()
            if n == 10:
                turn_extremes(0, 2, maxs)
                bring_out(0, 2)
                turn_extremes(0, 1, mins)
                bring_out(0, 1)
            if n == 11:
                variances_of_summed(0, P)
                turn_means(0)
                bring_out(0, 0)
                for slot in (2, 1):
                    add_target_gpsimd(0, slot)
            if n == 12:
                clamp_summed(0, P)
                add_target_gpsimd(0, 0)
            if n == 13:
                finish_std(0)
                store(0, slice(0, 4))
        c = NCH - 1
        finish_tiles(1)
        extremes(c, 1, ALU.max, maxs)
        sums(c, 1)
        extremes(c, 1, ALU.min, mins)
        extremes(c, 0, ALU.max, maxs)
        turn_extremes(1, 2, maxs)
        extremes(c, 0, ALU.min, mins)
        turn_extremes(1, 1, mins)
        means_of_summed(1, LAST)
        sums(c, 0)
        variances_of_summed(1, LAST)
        rest(1, LAST)
        add_target(1, 2)
        clamp_summed(1, LAST)
        turn_means(1)
        finish_std(1)
        add_target(1, 1)
        store(1, slice(1, 3))
        add_target(1, 0)
        store(1, slice(0, 1))
        store(1, slice(3, 4))
